import numpy as np
import ml_dtypes


def mxq(x, axis, fmt="e4m3"):
    dtype, down = {"e4m3": (ml_dtypes.float8_e4m3fn, 7), "e5m2": (ml_dtypes.float8_e5m2, 14)}[fmt]
    v = np.moveaxis(np.asarray(x, np.float32).astype(ml_dtypes.bfloat16).astype(np.float64), axis, -1)
    blocks = v.reshape(v.shape[:-1] + (-1, 32))
    amax = np.abs(blocks).max(-1, keepdims=True)
    byte = np.maximum(np.where(amax > 0, np.frexp(amax)[1] - 1 + 127, 0) - down, 1)
    scale = np.exp2(byte - 127.0)
    codes = (blocks / scale).astype(np.float32).astype(dtype).astype(np.float64)
    return np.moveaxis((codes * scale).reshape(v.shape), -1, axis)


WIDE = False


def mx_kscale(k):
    if not WIDE:
        return np.ones(k)
    levels = np.array([10, -10, 5, -5, 0])
    a = np.random.permutation(np.resize(levels, k // 512 * 4)).reshape(k // 512, 4)
    idx = np.arange(k)
    return np.exp2(a[idx // 512, idx % 128 // 32])


BF16 = ml_dtypes.bfloat16


def bf(x):
    return np.asarray(x, np.float32).astype(BF16)


def f64(x):
    return np.asarray(x).astype(np.float64)


E2M1 = np.array([0.0, 0.5, 1.0, 1.5, 2.0, 3.0, 4.0, 6.0, -0.0, -0.5, -1.0, -1.5, -2.0, -3.0, -4.0, -6.0])


def pack_weight(w, fmt):
    k, n = w.shape
    w = f64(bf(w)).reshape(k // 32, 32, n)
    amax = np.abs(w).max(1)
    if fmt == "e4m3":
        byte = np.frexp(amax)[1] - 1 + 127 - 7
    else:
        mant, ex = np.frexp(amax / 6.0)
        byte = np.where(mant > 0.5, ex, ex - 1) + 127
    byte = np.clip(np.where(amax > 0, byte, 1), 1, 254)
    scaled = (w * np.exp2(127.0 - byte)[:, None, :]).reshape(k, n).astype(np.float32)
    by_word = np.ascontiguousarray(scaled.reshape(k // 512, 128, 4, n).transpose(0, 1, 3, 2))
    if fmt == "e4m3":
        words = by_word.astype(ml_dtypes.float8_e4m3fn).view(np.uint8)
    else:
        c = by_word.astype(ml_dtypes.float4_e2m1fn).view(np.uint8) & 0xF
        words = c[..., 0::2] | (c[..., 1::2] << 4)
    return np.ascontiguousarray(words), np.ascontiguousarray(byte.astype(np.uint8).reshape(k // 512, 16, n))


def unpack_weight(words, scales, fmt):
    g, p, n, _ = words.shape
    if fmt == "e4m3":
        vals = np.ascontiguousarray(words).view(ml_dtypes.float8_e4m3fn).astype(np.float64)
    else:
        nib = np.empty((g, p, n, 4), np.uint8)
        nib[..., 0::2] = words & 0xF
        nib[..., 1::2] = words >> 4
        vals = E2M1[nib]
    vals = vals * np.repeat(np.exp2(scales.astype(np.float64) - 127.0), 8, axis=1)[..., None]
    return vals.transpose(0, 1, 3, 2).reshape(g * 512, n)


T, S, B, E, Z = 640, 8192, 1, 512, 128


def silu(v):
    return v / (1.0 + np.exp(-v))


def setup_inputs():
    s, t = mx_kscale(E), mx_kscale(E)
    q_scaled = bf(np.random.standard_normal((T, B, Z)) * 1.5 / np.sqrt(Z))
    k = bf(np.random.standard_normal((S, B, Z)) * 1.5)
    key = bf(np.random.standard_normal((S, B, E)) * s)
    query = bf(np.random.standard_normal((T, B, E)) * t)
    Wv = np.random.standard_normal((E, E)) / np.sqrt(E) / s[None, :]
    Wv_words, Wv_scales = pack_weight(np.ascontiguousarray(Wv.T), "e4m3")
    bv = bf(np.random.standard_normal(E) * 0.3)
    Wr = np.random.standard_normal((E, E)) / np.sqrt(E) / t[None, :]
    Wr_words, Wr_scales = pack_weight(np.ascontiguousarray(Wr.T), "e4m3")
    br = bf(np.random.standard_normal(E) * 0.3)
    return {"q_scaled": q_scaled,
            "k": k,
            "key": key,
            "query": query,
            "Wv_words": Wv_words,
            "Wv_scales": Wv_scales,
            "bv": bv,
            "Wr_words": Wr_words,
            "Wr_scales": Wr_scales,
            "br": br}


def reference(q_scaled, k, key, query, Wv_words, Wv_scales, bv, Wr_words, Wr_scales, br):
    v = silu((mxq(f64(key), 2, "e4m3") @ unpack_weight(Wv_words, Wv_scales, "e4m3")) + f64(bv))
    r = silu((mxq(f64(query), 2, "e4m3") @ unpack_weight(Wr_words, Wr_scales, "e4m3")) + f64(br))
    qk = f64(q_scaled).transpose(1, 0, 2) @ f64(k).transpose(1, 2, 0)
    e = np.exp(qk - qk.max(-1, keepdims=True))
    h = (mxq(e, 2, "e4m3") @ mxq(v.transpose(1, 0, 2), 1, "e4m3")) / e.sum(-1, keepdims=True)
    return h.transpose(1, 0, 2) * r

@@ -1,0 +1,378 @@
+from contextlib import ExitStack
+
+import concourse.mybir as mybir
+from concourse.masks import make_identity
+
+F32 = mybir.dt.float32
+BF16 = mybir.dt.bfloat16
+I32 = mybir.dt.int32
+U32 = mybir.dt.uint32
+U8 = mybir.dt.uint8
+FP8X4 = mybir.dt.float8_e4m3fn_x4
+ALU = mybir.AluOpType
+FUNC = mybir.ActivationFunctionType
+AXIS = mybir.AxisListType
+
+P = 128
+PACK = 4
+K_PASS = P * PACK
+
+T, S, E, Z = 640, 8192, 512, 128
+T_TILES = T // P
+GROUPS = S // K_PASS
+E_WORDS = E // 2
+N_BLOCKS = E // P
+CHUNK_GROUPS = 4
+CHUNK = CHUNK_GROUPS * K_PASS
+CHUNKS_PER_TILE = GROUPS // CHUNK_GROUPS
+CHUNKS = T_TILES * CHUNKS_PER_TILE
+BANK_GROUPS = 2
+
+FLOPS = 2 * (S * E * E + T * E * E + T * S * Z + T * S * E)
+
+
+def load_weight(nc, pool, words, scales, label):
+    codes = pool.tile([P, E], U32, name=label + "_codes", align_bytes=64)
+    plane = pool.tile([P, E], U8, name=label + "_plane", align_bytes=64)
+    nc.vector.memset(plane[:].bitcast(I32), 0)
+    scale_rows = scales.rearrange("g q n -> (g q) n").bitcast(I32)
+    for quadrant in range(4):
+        nc.sync.dma_start(
+            out=plane[32 * quadrant : 32 * quadrant + 4, :].bitcast(I32),
+            in_=scale_rows[4 * quadrant : 4 * quadrant + 4, :],
+        )
+    nc.sync.dma_start(out=codes[:].bitcast(I32), in_=words.rearrange("g p n t -> (g p) (n t)").bitcast(I32))
+    return codes, plane
+
+
+def features_onto_partitions(nc, psum, identity_f32, rows, grouped, n_tiles):
+    row_words = rows[:].bitcast(F32)
+    grouped_words = grouped[:].bitcast(F32)
+    for first in range(0, n_tiles, 2):
+        count = min(2, n_tiles - first)
+        turned = psum.tile([P, 2, 2, P], F32, tag="turned")
+        for a in range(count):
+            for u in range(2):
+                nc.tensor.transpose(turned[:, a, u, :], row_words[:, first + a, u:E_WORDS:2], identity_f32[:])
+        nc.scalar.copy(
+            out=grouped_words[:, first : first + count, :, :],
+            in_=turned[:, 0:count, :, :].rearrange("p a u r -> p a r u"),
+        )
+
+
+def tile_gatedcrossattention_pa_k_kernel(
+    tc, q_scaled, k, key, query, Wv_words, Wv_scales, bv, Wr_words, Wr_scales, br, out
+):
+    nc = tc.nc
+    key_groups = key.rearrange("(g p j) b e -> g p j (b e)", p=P, j=PACK)
+    k_groups = k.rearrange("(g p j) b z -> p g (j b z)", p=P, j=PACK)
+    q_tiles = q_scaled.rearrange("(i p) b z -> p i (b z)", p=P)
+    query_tiles = query.rearrange("(i p) b e -> p i (b e)", p=P)
+    out_tiles = out.rearrange("(i p) b n -> i p (b n)", p=P)
+
+    with ExitStack() as whole:
+        const = whole.enter_context(tc.tile_pool(name="const", bufs=1))
+        keep = whole.enter_context(tc.tile_pool(name="keep", bufs=1))
+        score_pool = whole.enter_context(tc.tile_pool(name="score_pool", bufs=2))
+        score_psum = whole.enter_context(tc.psum_pool(name="score_psum", bufs=2))
+
+        identity_f32 = const.tile([P, P], F32)
+        make_identity(nc, identity_f32[:])
+        identity_bf16 = const.tile([P, P], BF16)
+        make_identity(nc, identity_bf16[:])
+        bias_v = const.tile([P, E], BF16)
+        bias_r = const.tile([P, E], BF16)
+
+        k_turned = keep.tile([P, S], BF16)
+        q_turned = keep.tile([P, T], BF16)
+        v_codes = keep.tile([P, GROUPS, E], U32, align_bytes=64)
+        v_plane = keep.tile([P, GROUPS, E], U8, align_bytes=64)
+        gate = keep.tile([P, T_TILES, E], F32)
+
+        scores = {}
+        group_max = {}
+        neg_max = {}
+
+        def score_group(i, g):
+            if g == 0:
+                score_rows = score_pool.tile([P, S], F32)
+                scores[i] = score_rows
+                maxima = score_pool.tile([P, GROUPS], F32)
+                group_max[i] = maxima
+            bank = score_psum.tile([P, K_PASS], F32)
+            nc.tensor.matmul(
+                out=bank[:],
+                lhsT=q_turned[:, i * P : (i + 1) * P],
+                rhs=k_turned[:, g * K_PASS : (g + 1) * K_PASS],
+                start=True,
+                stop=True,
+            )
+            nc.vector.tensor_scalar(
+                out=scores[i][:, g * K_PASS : (g + 1) * K_PASS],
+                in0=bank[:],
+                scalar1=1.0,
+                scalar2=None,
+                op0=ALU.mult,
+                op1=ALU.max,
+                accum_out=group_max[i][:, g : g + 1],
+            )
+            if g == GROUPS - 1:
+                minus_max = score_pool.tile([P, 1], F32)
+                nc.vector.tensor_reduce(out=minus_max[:], in_=group_max[i][:], axis=AXIS.X, op=ALU.max, negate=True)
+                neg_max[i] = minus_max
+
+        with ExitStack() as value_phase:
+            stage = value_phase.enter_context(tc.tile_pool(name="stage", bufs=2))
+            turn_psum = value_phase.enter_context(tc.psum_pool(name="turn_psum", bufs=2))
+            product_psum = value_phase.enter_context(tc.psum_pool(name="product_psum", bufs=4))
+
+            key_rows = {}
+            key_grouped = {}
+            key_codes = {}
+            key_plane = {}
+            v_f32 = {}
+            v_grouped = {}
+
+            def load_key(g):
+                rows = stage.tile([P, PACK, E], BF16, bufs=4)
+                nc.sync.dma_start(out=rows[:], in_=key_groups[g])
+                key_rows[g] = rows
+
+            def turn_key(g):
+                grouped = stage.tile([P, PACK, P, PACK], BF16, tag="key_grouped", align_bytes=64)
+                features_onto_partitions(nc, turn_psum, identity_f32, key_rows[g], grouped, PACK)
+                key_grouped[g] = grouped
+
+            def quantise_key(g):
+                codes = stage.tile([P, K_PASS], U32, align_bytes=64)
+                plane = stage.tile([P, K_PASS], U8, align_bytes=64)
+                nc.vector.quantize_mx(
+                    out=codes[:].bitcast(FP8X4),
+                    scales=plane[:],
+                    in_=key_grouped[g][:].rearrange("p j r t -> p (j r t)"),
+                )
+                key_codes[g] = codes
+                key_plane[g] = plane
+
+            def turn_k(g):
+                turned = turn_psum.tile([P, PACK, P], BF16, tag="turned")
+                for j in range(PACK):
+                    nc.tensor.transpose(turned[:, j, :], k_rows[:, g, j * Z : (j + 1) * Z], identity_bf16[:])
+                nc.scalar.copy(
+                    out=k_turned[:, g * K_PASS : (g + 1) * K_PASS], in_=turned[:].rearrange("p j r -> p (j r)")
+                )
+
+            def value_products(g):
+                summed = stage.tile([P, N_BLOCKS, P, PACK], F32)
+                for nb in range(N_BLOCKS):
+                    features = slice(nb * P, (nb + 1) * P)
+                    product = product_psum.tile([P, PACK, P], F32)
+                    for j in range(PACK):
+                        slot = slice(j * P, (j + 1) * P)
+                        nc.tensor.matmul_mx(
+                            out=product[:, j, :],
+                            lhsT=key_codes[g][:, slot].bitcast(FP8X4),
+                            lhsT_scale=key_plane[g][:, slot],
+                            rhs=wv_codes[:, features].bitcast(FP8X4),
+                            rhs_scale=wv_plane[:, features],
+                            start=True,
+                            stop=True,
+                        )
+                    nc.vector.tensor_tensor(
+                        out=summed[:, nb, :, :],
+                        in0=product[:].rearrange("p j n -> p n j"),
+                        in1=bias_v[:, features].unsqueeze(2).to_broadcast([P, P, PACK]),
+                        op=ALU.add,
+                    )
+                v_f32[g] = summed
+
+            def value_silu(g):
+                grouped = stage.tile([P, E * PACK], BF16, tag="v_grouped", align_bytes=64)
+                nc.scalar.activation(
+                    out=grouped[:], in_=v_f32[g][:].rearrange("p b n j -> p (b n j)"), func=FUNC.Silu
+                )
+                v_grouped[g] = grouped
+
+            def quantise_value(g):
+                nc.vector.quantize_mx(out=v_codes[:, g, :].bitcast(FP8X4), scales=v_plane[:, g, :], in_=v_grouped[g][:])
+
+            def gate_tile(i):
+                queries = slice(i * P, (i + 1) * P)
+                product = product_psum.tile([P, E], F32, tag="product")
+                nc.tensor.matmul_mx(
+                    out=product[:],
+                    lhsT=query_codes[:, queries].bitcast(FP8X4),
+                    lhsT_scale=query_plane[:, queries],
+                    rhs=wr_codes[:].bitcast(FP8X4),
+                    rhs_scale=wr_plane[:],
+                    start=True,
+                    stop=True,
+                )
+                summed = stage.tile([P, E], F32, tag="gate_sum")
+                nc.vector.tensor_tensor(out=summed[:], in0=product[:], in1=bias_r[:], op=ALU.add)
+                nc.scalar.activation(out=gate[:, i, :], in_=summed[:], func=FUNC.Silu)
+
+            load_key(0)
+            wv_codes, wv_plane = load_weight(nc, const, Wv_words, Wv_scales, "wv")
+            load_key(1)
+            query_rows = stage.tile([P, T_TILES, E], BF16, bufs=1)
+            nc.sync.dma_start(out=query_rows[:], in_=query_tiles)
+            wr_codes, wr_plane = load_weight(nc, const, Wr_words, Wr_scales, "wr")
+            load_key(2)
+            load_key(3)
+            nc.gpsimd.dma_start(out=bias_v[:], in_=bv.partition_broadcast(P))
+            q_rows = stage.tile([P, T_TILES, Z], BF16, bufs=1)
+            nc.gpsimd.dma_start(out=q_rows[:], in_=q_tiles)
+            k_rows = stage.tile([P, GROUPS, PACK * Z], BF16, bufs=1)
+            for first in range(0, GROUPS, CHUNK_GROUPS):
+                nc.gpsimd.dma_start(
+                    out=k_rows[:, first : first + CHUNK_GROUPS, :], in_=k_groups[:, first : first + CHUNK_GROUPS, :]
+                )
+            nc.gpsimd.dma_start(out=bias_r[:], in_=br.partition_broadcast(P))
+
+            turn_key(0)
+            turn_key(1)
+            quantise_key(0)
+            query_grouped = stage.tile([P, T_TILES, P, PACK], BF16, bufs=1, align_bytes=64)
+            features_onto_partitions(nc, turn_psum, identity_f32, query_rows, query_grouped, T_TILES)
+            query_codes = stage.tile([P, T], U32, bufs=1, align_bytes=64)
+            query_plane = stage.tile([P, T], U8, bufs=1, align_bytes=64)
+            for first, count in ((0, 4), (4, 1)):
+                nc.vector.quantize_mx(
+                    out=query_codes[:, first * P : (first + count) * P].bitcast(FP8X4),
+                    scales=query_plane[:, first * P : (first + count) * P],
+                    in_=query_grouped[:, first : first + count, :, :].rearrange("p a r t -> p (a r t)"),
+                )
+            q_bank = turn_psum.tile([P, T_TILES, P], BF16, tag="turned")
+            for i in range(T_TILES):
+                nc.tensor.transpose(q_bank[:, i, :], q_rows[:, i, :], identity_bf16[:])
+            nc.scalar.copy(out=q_turned[:], in_=q_bank[:].rearrange("p i r -> p (i r)"))
+            turn_k(0)
+            turn_k(1)
+
+            for n in range(GROUPS + 1):
+                if n < GROUPS:
+                    value_products(n)
+                if n >= 1:
+                    value_silu(n - 1)
+                if n + 1 < GROUPS:
+                    quantise_key(n + 1)
+                if n < GROUPS:
+                    score_group(0, n)
+                if n < T_TILES:
+                    gate_tile(n)
+                if n + 4 < GROUPS:
+                    load_key(n + 4)
+                if n + 2 < GROUPS:
+                    turn_key(n + 2)
+                    turn_k(n + 2)
+                if n >= 1:
+                    quantise_value(n - 1)
+
+        with ExitStack() as softmax_phase:
+            work = softmax_phase.enter_context(tc.tile_pool(name="work", bufs=3, reuse_waits="tile"))
+            e_psum = softmax_phase.enter_context(tc.psum_pool(name="e_psum", bufs=4, reuse_waits="tile"))
+            h_psum = softmax_phase.enter_context(tc.psum_pool(name="h_psum", bufs=2, reuse_waits="tile"))
+
+            e_rows = {}
+            e_grouped = {}
+            e_codes = {}
+            e_plane = {}
+            chunk_sum = {}
+            h_bank = {}
+
+            def exp_chunk(m):
+                i, c = divmod(m, CHUNKS_PER_TILE)
+                if c == 0:
+                    sums = work.tile([P, CHUNKS_PER_TILE], F32, bufs=2)
+                    chunk_sum[i] = sums
+                rows = work.tile([P, CHUNK], BF16)
+                nc.scalar.activation(
+                    out=rows[:],
+                    in_=scores[i][:, c * CHUNK : (c + 1) * CHUNK],
+                    func=FUNC.Exp,
+                    bias=neg_max[i][:, 0:1],
+                    scale=1.0,
+                    accum_out=chunk_sum[i][:, c : c + 1],
+                )
+                e_rows[m] = rows
+
+            def turn_e(m, scores_left):
+                grouped = work.tile([P, CHUNK_GROUPS, P, PACK], BF16, align_bytes=64)
+                for bank_index in range(CHUNK_GROUPS // BANK_GROUPS):
+                    first = bank_index * BANK_GROUPS
+                    turned = e_psum.tile([P, BANK_GROUPS, PACK, P], BF16)
+                    for a in range(BANK_GROUPS):
+                        for j in range(PACK):
+                            column = ((first + a) * PACK + j) * P
+                            nc.tensor.transpose(turned[:, a, j, :], e_rows[m][:, column : column + P], identity_bf16[:])
+                    to_vector = bank_index == 1 and (m % 2 == 1 or not scores_left)
+                    copy = nc.vector.tensor_copy if to_vector else nc.scalar.copy
+                    copy(
+                        out=grouped[:, first : first + BANK_GROUPS, :, :],
+                        in_=turned[:].rearrange("p a j r -> p a r j"),
+                    )
+                e_grouped[m] = grouped
+
+            def quantise_e(m):
+                i, c = divmod(m, CHUNKS_PER_TILE)
+                if c == 0:
+                    codes = work.tile([P, GROUPS * P], U32, bufs=2, align_bytes=64)
+                    plane = work.tile([P, GROUPS * P], U8, bufs=2, align_bytes=64)
+                    e_codes[i] = codes
+                    e_plane[i] = plane
+                columns = slice(c * CHUNK_GROUPS * P, (c + 1) * CHUNK_GROUPS * P)
+                nc.vector.quantize_mx(
+                    out=e_codes[i][:, columns].bitcast(FP8X4),
+                    scales=e_plane[i][:, columns],
+                    in_=e_grouped[m][:].rearrange("p a r j -> p (a r j)"),
+                )
+
+            def attend(m):
+                i, c = divmod(m, CHUNKS_PER_TILE)
+                if c == 0:
+                    bank = h_psum.tile([P, E], F32)
+                    h_bank[i] = bank
+                for g in range(c * CHUNK_GROUPS, (c + 1) * CHUNK_GROUPS):
+                    queries = slice(g * P, (g + 1) * P)
+                    nc.tensor.matmul_mx(
+                        out=h_bank[i][:],
+                        lhsT=e_codes[i][:, queries].bitcast(FP8X4),
+                        lhsT_scale=e_plane[i][:, queries],
+                        rhs=v_codes[:, g, :].bitcast(FP8X4),
+                        rhs_scale=v_plane[:, g, :],
+                        start=(g == 0),
+                        stop=(g == GROUPS - 1),
+                    )
+
+            def finish_tile(i):
+                row_sum = work.tile([P, 1], F32)
+                nc.vector.tensor_reduce(out=row_sum[:], in_=chunk_sum[i][:], axis=AXIS.X, op=ALU.add)
+                inverse = work.tile([P, 1], F32)
+                nc.vector.reciprocal(out=inverse[:], in_=row_sum[:])
+                result = work.tile([P, E], F32, bufs=2)
+                nc.vector.scalar_tensor_tensor(
+                    out=result[:], in0=h_bank[i][:], scalar=inverse[:, 0:1], in1=gate[:, i, :], op0=ALU.mult, op1=ALU.mult
+                )
+                nc.sync.dma_start(out=out_tiles[i], in_=result[:])
+
+            for m in range(CHUNKS + 2):
+                next_tile, c = divmod(m, CHUNKS_PER_TILE)
+                next_tile += 1
+                scores_left = next_tile < T_TILES
+                if scores_left:
+                    score_group(next_tile, c * CHUNK_GROUPS)
+                    score_group(next_tile, c * CHUNK_GROUPS + 1)
+                if m < CHUNKS:
+                    exp_chunk(m)
+                if 1 <= m <= CHUNKS:
+                    turn_e(m - 1, scores_left)
+                if m >= 2:
+                    quantise_e(m - 2)
+                if scores_left:
+                    score_group(next_tile, c * CHUNK_GROUPS + 2)
+                    score_group(next_tile, c * CHUNK_GROUPS + 3)
+                if m >= 2:
+                    attend(m - 2)
+                    if (m - 2) % CHUNKS_PER_TILE == CHUNKS_PER_TILE - 1:
+                        finish_tile((m - 2) // CHUNKS_PER_TILE)

@@ -27,6 +27,8 @@ CHUNK = CHUNK_GROUPS * K_PASS
 CHUNKS_PER_TILE = GROUPS // CHUNK_GROUPS
 CHUNKS = T_TILES * CHUNKS_PER_TILE
 BANK_GROUPS = 2
+CHUNK_BANKS = CHUNK_GROUPS // BANK_GROUPS
+GATE_LAG = 2
 
 FLOPS = 2 * (S * E * E + T * E * E + T * S * Z + T * S * E)
 
@@ -43,6 +45,17 @@ def load_weight(nc, pool, words, scales, label):
         )
     nc.sync.dma_start(out=codes[:].bitcast(I32), in_=words.rearrange("g p n t -> (g p) (n t)").bitcast(I32))
     return codes, plane
+
+
+def spread_bias(nc, pool, psum, ones, bias, label):
+    rows = pool.tile([P, E], BF16, name=label + "_rows")
+    nc.vector.memset(rows[:], 0.0)
+    nc.sync.dma_start(out=rows[0:1, :], in_=bias.unsqueeze(0))
+    bank = psum.tile([P, E], F32, tag="product")
+    nc.tensor.matmul(out=bank[:], lhsT=ones[:], rhs=rows[:], start=True, stop=True)
+    spread = pool.tile([P, E], F32, name=label)
+    nc.scalar.copy(out=spread[:], in_=bank[:])
+    return spread
 
 
 def features_onto_partitions(nc, psum, identity_f32, rows, grouped, n_tiles):
@@ -75,13 +88,14 @@ def tile_gatedcrossattention_pa_k_kernel(
         keep = whole.enter_context(tc.tile_pool(name="keep", bufs=1))
         score_pool = whole.enter_context(tc.tile_pool(name="score_pool", bufs=2))
         score_psum = whole.enter_context(tc.psum_pool(name="score_psum", bufs=2))
+        whole.enter_context(tc.manual_schedule())
 
         identity_f32 = const.tile([P, P], F32)
         make_identity(nc, identity_f32[:])
         identity_bf16 = const.tile([P, P], BF16)
         make_identity(nc, identity_bf16[:])
-        bias_v = const.tile([P, E], BF16)
-        bias_r = const.tile([P, E], BF16)
+        ones = const.tile([P, P], BF16)
+        nc.vector.memset(ones[:], 1.0)
 
         k_turned = keep.tile([P, S], BF16)
         q_turned = keep.tile([P, T], BF16)
@@ -132,6 +146,7 @@ def tile_gatedcrossattention_pa_k_kernel(
             key_plane = {}
             v_f32 = {}
             v_grouped = {}
+            gate_f32 = {}
 
             def load_key(g):
                 rows = stage.tile([P, PACK, E], BF16, bufs=4)
@@ -161,6 +176,21 @@ def tile_gatedcrossattention_pa_k_kernel(
                 nc.scalar.copy(
                     out=k_turned[:, g * K_PASS : (g + 1) * K_PASS], in_=turned[:].rearrange("p j r -> p (j r)")
                 )
+
+            def turn_queries():
+                q_bank = turn_psum.tile([P, T_TILES, P], BF16, tag="turned")
+                for i in range(T_TILES):
+                    nc.tensor.transpose(q_bank[:, i, :], q_rows[:, i, :], identity_bf16[:])
+                nc.scalar.copy(out=q_turned[:], in_=q_bank[:].rearrange("p i r -> p (i r)"))
+                features_onto_partitions(nc, turn_psum, identity_f32, query_rows, query_grouped, T_TILES)
+
+            def quantise_query():
+                for first, count in ((0, 4), (4, 1)):
+                    nc.vector.quantize_mx(
+                        out=query_codes[:, first * P : (first + count) * P].bitcast(FP8X4),
+                        scales=query_plane[:, first * P : (first + count) * P],
+                        in_=query_grouped[:, first : first + count, :, :].rearrange("p a r t -> p (a r t)"),
+                    )
 
             def value_products(g):
                 summed = stage.tile([P, N_BLOCKS, P, PACK], F32)
@@ -196,7 +226,7 @@ def tile_gatedcrossattention_pa_k_kernel(
             def quantise_value(g):
                 nc.vector.quantize_mx(out=v_codes[:, g, :].bitcast(FP8X4), scales=v_plane[:, g, :], in_=v_grouped[g][:])
 
-            def gate_tile(i):
+            def gate_products(i):
                 queries = slice(i * P, (i + 1) * P)
                 product = product_psum.tile([P, E], F32, tag="product")
                 nc.tensor.matmul_mx(
@@ -210,17 +240,21 @@ def tile_gatedcrossattention_pa_k_kernel(
                 )
                 summed = stage.tile([P, E], F32, tag="gate_sum")
                 nc.vector.tensor_tensor(out=summed[:], in0=product[:], in1=bias_r[:], op=ALU.add)
-                nc.scalar.activation(out=gate[:, i, :], in_=summed[:], func=FUNC.Silu)
+                gate_f32[i] = summed
 
+            def gate_silu(i):
+                nc.scalar.activation(out=gate[:, i, :], in_=gate_f32[i][:], func=FUNC.Silu)
+
+            bias_v = spread_bias(nc, const, product_psum, ones, bv, "bias_v")
+            bias_r = spread_bias(nc, const, product_psum, ones, br, "bias_r")
             load_key(0)
             wv_codes, wv_plane = load_weight(nc, const, Wv_words, Wv_scales, "wv")
             load_key(1)
+            load_key(2)
             query_rows = stage.tile([P, T_TILES, E], BF16, bufs=1)
             nc.sync.dma_start(out=query_rows[:], in_=query_tiles)
             wr_codes, wr_plane = load_weight(nc, const, Wr_words, Wr_scales, "wr")
-            load_key(2)
             load_key(3)
-            nc.gpsimd.dma_start(out=bias_v[:], in_=bv.partition_broadcast(P))
             q_rows = stage.tile([P, T_TILES, Z], BF16, bufs=1)
             nc.gpsimd.dma_start(out=q_rows[:], in_=q_tiles)
             k_rows = stage.tile([P, GROUPS, PACK * Z], BF16, bufs=1)
@@ -228,44 +262,36 @@ def tile_gatedcrossattention_pa_k_kernel(
                 nc.gpsimd.dma_start(
                     out=k_rows[:, first : first + CHUNK_GROUPS, :], in_=k_groups[:, first : first + CHUNK_GROUPS, :]
                 )
-            nc.gpsimd.dma_start(out=bias_r[:], in_=br.partition_broadcast(P))
+            query_grouped = stage.tile([P, T_TILES, P, PACK], BF16, bufs=1, align_bytes=64)
+            query_codes = stage.tile([P, T], U32, bufs=1, align_bytes=64)
+            query_plane = stage.tile([P, T], U8, bufs=1, align_bytes=64)
 
             turn_key(0)
             turn_key(1)
             quantise_key(0)
-            query_grouped = stage.tile([P, T_TILES, P, PACK], BF16, bufs=1, align_bytes=64)
-            features_onto_partitions(nc, turn_psum, identity_f32, query_rows, query_grouped, T_TILES)
-            query_codes = stage.tile([P, T], U32, bufs=1, align_bytes=64)
-            query_plane = stage.tile([P, T], U8, bufs=1, align_bytes=64)
-            for first, count in ((0, 4), (4, 1)):
-                nc.vector.quantize_mx(
-                    out=query_codes[:, first * P : (first + count) * P].bitcast(FP8X4),
-                    scales=query_plane[:, first * P : (first + count) * P],
-                    in_=query_grouped[:, first : first + count, :, :].rearrange("p a r t -> p (a r t)"),
-                )
-            q_bank = turn_psum.tile([P, T_TILES, P], BF16, tag="turned")
-            for i in range(T_TILES):
-                nc.tensor.transpose(q_bank[:, i, :], q_rows[:, i, :], identity_bf16[:])
-            nc.scalar.copy(out=q_turned[:], in_=q_bank[:].rearrange("p i r -> p (i r)"))
-            turn_k(0)
-            turn_k(1)
-
             for n in range(GROUPS + 1):
                 if n < GROUPS:
                     value_products(n)
+                if GATE_LAG <= n < GATE_LAG + T_TILES:
+                    gate_products(n - GATE_LAG)
                 if n >= 1:
                     value_silu(n - 1)
+                if GATE_LAG + 1 <= n < GATE_LAG + 1 + T_TILES:
+                    gate_silu(n - GATE_LAG - 1)
                 if n + 1 < GROUPS:
                     quantise_key(n + 1)
-                if n < GROUPS:
-                    score_group(0, n)
-                if n < T_TILES:
-                    gate_tile(n)
+                if n >= 1:
+                    score_group(0, n - 1)
                 if n + 4 < GROUPS:
                     load_key(n + 4)
                 if n + 2 < GROUPS:
                     turn_key(n + 2)
-                    turn_k(n + 2)
+                if n == 0:
+                    turn_queries()
+                if n < GROUPS:
+                    turn_k(n)
+                if n == 1:
+                    quantise_query()
                 if n >= 1:
                     quantise_value(n - 1)
 
@@ -275,10 +301,12 @@ def tile_gatedcrossattention_pa_k_kernel(
             h_psum = softmax_phase.enter_context(tc.psum_pool(name="h_psum", bufs=2, reuse_waits="tile"))
 
             e_rows = {}
+            e_banks = {}
             e_grouped = {}
             e_codes = {}
             e_plane = {}
             chunk_sum = {}
+            inverse_sum = {}
             h_bank = {}
 
             def exp_chunk(m):
@@ -297,20 +325,30 @@ def tile_gatedcrossattention_pa_k_kernel(
                 )
                 e_rows[m] = rows
 
-            def turn_e(m, scores_left):
-                grouped = work.tile([P, CHUNK_GROUPS, P, PACK], BF16, align_bytes=64)
-                for bank_index in range(CHUNK_GROUPS // BANK_GROUPS):
-                    first = bank_index * BANK_GROUPS
+            def invert_sum(i):
+                row_sum = work.tile([P, 1], F32)
+                nc.vector.tensor_reduce(out=row_sum[:], in_=chunk_sum[i][:], axis=AXIS.X, op=ALU.add)
+                inverse = work.tile([P, 1], F32)
+                nc.vector.reciprocal(out=inverse[:], in_=row_sum[:])
+                inverse_sum[i] = inverse
+
+            def turn_e(m):
+                for b in range(CHUNK_BANKS):
                     turned = e_psum.tile([P, BANK_GROUPS, PACK, P], BF16)
                     for a in range(BANK_GROUPS):
                         for j in range(PACK):
-                            column = ((first + a) * PACK + j) * P
+                            column = ((b * BANK_GROUPS + a) * PACK + j) * P
                             nc.tensor.transpose(turned[:, a, j, :], e_rows[m][:, column : column + P], identity_bf16[:])
-                    to_vector = bank_index == 1 and (m % 2 == 1 or not scores_left)
+                    e_banks[m, b] = turned
+
+            def group_e(m, scores_left):
+                grouped = work.tile([P, CHUNK_GROUPS, P, PACK], BF16, align_bytes=64)
+                for b in range(CHUNK_BANKS):
+                    to_vector = (b == 1 and m % 2 == 1) or not scores_left
                     copy = nc.vector.tensor_copy if to_vector else nc.scalar.copy
                     copy(
-                        out=grouped[:, first : first + BANK_GROUPS, :, :],
-                        in_=turned[:].rearrange("p a j r -> p a r j"),
+                        out=grouped[:, b * BANK_GROUPS : (b + 1) * BANK_GROUPS, :, :],
+                        in_=e_banks[m, b][:].rearrange("p a j r -> p a r j"),
                     )
                 e_grouped[m] = grouped
 
@@ -346,17 +384,18 @@ def tile_gatedcrossattention_pa_k_kernel(
                     )
 
             def finish_tile(i):
-                row_sum = work.tile([P, 1], F32)
-                nc.vector.tensor_reduce(out=row_sum[:], in_=chunk_sum[i][:], axis=AXIS.X, op=ALU.add)
-                inverse = work.tile([P, 1], F32)
-                nc.vector.reciprocal(out=inverse[:], in_=row_sum[:])
                 result = work.tile([P, E], F32, bufs=2)
                 nc.vector.scalar_tensor_tensor(
-                    out=result[:], in0=h_bank[i][:], scalar=inverse[:, 0:1], in1=gate[:, i, :], op0=ALU.mult, op1=ALU.mult
+                    out=result[:],
+                    in0=h_bank[i][:],
+                    scalar=inverse_sum[i][:, 0:1],
+                    in1=gate[:, i, :],
+                    op0=ALU.mult,
+                    op1=ALU.mult,
                 )
                 nc.sync.dma_start(out=out_tiles[i], in_=result[:])
 
-            for m in range(CHUNKS + 2):
+            for m in range(CHUNKS + 3):
                 next_tile, c = divmod(m, CHUNKS_PER_TILE)
                 next_tile += 1
                 scores_left = next_tile < T_TILES
@@ -366,13 +405,17 @@ def tile_gatedcrossattention_pa_k_kernel(
                 if m < CHUNKS:
                     exp_chunk(m)
                 if 1 <= m <= CHUNKS:
-                    turn_e(m - 1, scores_left)
-                if m >= 2:
-                    quantise_e(m - 2)
+                    turn_e(m - 1)
                 if scores_left:
                     score_group(next_tile, c * CHUNK_GROUPS + 2)
                     score_group(next_tile, c * CHUNK_GROUPS + 3)
-                if m >= 2:
-                    attend(m - 2)
-                    if (m - 2) % CHUNKS_PER_TILE == CHUNKS_PER_TILE - 1:
-                        finish_tile((m - 2) // CHUNKS_PER_TILE)
+                if 1 <= m <= CHUNKS:
+                    group_e(m - 1, scores_left)
+                    if c == 0:
+                        invert_sum(next_tile - 2)
+                if 2 <= m <= CHUNKS + 1:
+                    quantise_e(m - 2)
+                if m >= 3:
+                    attend(m - 3)
+                    if (m - 3) % CHUNKS_PER_TILE == CHUNKS_PER_TILE - 1:
+                        finish_tile((m - 3) // CHUNKS_PER_TILE)

@@ -26,8 +26,6 @@ CHUNK_GROUPS = 4
 CHUNK = CHUNK_GROUPS * K_PASS
 CHUNKS_PER_TILE = GROUPS // CHUNK_GROUPS
 CHUNKS = T_TILES * CHUNKS_PER_TILE
-BANK_GROUPS = 2
-CHUNK_BANKS = CHUNK_GROUPS // BANK_GROUPS
 GATE_LAG = 2
 
 FLOPS = 2 * (S * E * E + T * E * E + T * S * Z + T * S * E)
@@ -87,7 +85,6 @@ def tile_gatedcrossattention_pa_k_kernel(
         const = whole.enter_context(tc.tile_pool(name="const", bufs=1))
         keep = whole.enter_context(tc.tile_pool(name="keep", bufs=1))
         score_pool = whole.enter_context(tc.tile_pool(name="score_pool", bufs=2))
-        score_psum = whole.enter_context(tc.psum_pool(name="score_psum", bufs=2))
         whole.enter_context(tc.manual_schedule())
 
         identity_f32 = const.tile([P, P], F32)
@@ -107,7 +104,7 @@ def tile_gatedcrossattention_pa_k_kernel(
         group_max = {}
         neg_max = {}
 
-        def score_group(i, g):
+        def score_group(score_psum, i, g):
             if g == 0:
                 score_rows = score_pool.tile([P, S], F32)
                 scores[i] = score_rows
@@ -139,6 +136,7 @@ def tile_gatedcrossattention_pa_k_kernel(
             stage = value_phase.enter_context(tc.tile_pool(name="stage", bufs=2))
             turn_psum = value_phase.enter_context(tc.psum_pool(name="turn_psum", bufs=2))
             product_psum = value_phase.enter_context(tc.psum_pool(name="product_psum", bufs=4))
+            early_score_psum = value_phase.enter_context(tc.psum_pool(name="early_score_psum", bufs=2))
 
             key_rows = {}
             key_grouped = {}
@@ -281,7 +279,7 @@ def tile_gatedcrossattention_pa_k_kernel(
                 if n + 1 < GROUPS:
                     quantise_key(n + 1)
                 if n >= 1:
-                    score_group(0, n - 1)
+                    score_group(early_score_psum, 0, n - 1)
                 if n + 4 < GROUPS:
                     load_key(n + 4)
                 if n + 2 < GROUPS:
@@ -298,7 +296,8 @@ def tile_gatedcrossattention_pa_k_kernel(
         with ExitStack() as softmax_phase:
             work = softmax_phase.enter_context(tc.tile_pool(name="work", bufs=3, reuse_waits="tile"))
             e_psum = softmax_phase.enter_context(tc.psum_pool(name="e_psum", bufs=4, reuse_waits="tile"))
-            h_psum = softmax_phase.enter_context(tc.psum_pool(name="h_psum", bufs=2, reuse_waits="tile"))
+            h_psum = softmax_phase.enter_context(tc.psum_pool(name="h_psum", bufs=1, reuse_waits="tile"))
+            score_psum = softmax_phase.enter_context(tc.psum_pool(name="score_psum", bufs=3, reuse_waits="tile"))
 
             e_rows = {}
             e_banks = {}
@@ -333,23 +332,19 @@ def tile_gatedcrossattention_pa_k_kernel(
                 inverse_sum[i] = inverse
 
             def turn_e(m):
-                for b in range(CHUNK_BANKS):
-                    turned = e_psum.tile([P, BANK_GROUPS, PACK, P], BF16)
-                    for a in range(BANK_GROUPS):
-                        for j in range(PACK):
-                            column = ((b * BANK_GROUPS + a) * PACK + j) * P
-                            nc.tensor.transpose(turned[:, a, j, :], e_rows[m][:, column : column + P], identity_bf16[:])
-                    e_banks[m, b] = turned
+                for a in range(CHUNK_GROUPS):
+                    turned = e_psum.tile([P, PACK, P], BF16)
+                    for j in range(PACK):
+                        column = (a * PACK + j) * P
+                        nc.tensor.transpose(turned[:, j, :], e_rows[m][:, column : column + P], identity_bf16[:])
+                    e_banks[m, a] = turned
 
             def group_e(m, scores_left):
                 grouped = work.tile([P, CHUNK_GROUPS, P, PACK], BF16, align_bytes=64)
-                for b in range(CHUNK_BANKS):
-                    to_vector = (b == 1 and m % 2 == 1) or not scores_left
+                for a in range(CHUNK_GROUPS):
+                    to_vector = a == CHUNK_GROUPS - 1 if scores_left else a > 0
                     copy = nc.vector.tensor_copy if to_vector else nc.scalar.copy
-                    copy(
-                        out=grouped[:, b * BANK_GROUPS : (b + 1) * BANK_GROUPS, :, :],
-                        in_=e_banks[m, b][:].rearrange("p a j r -> p a r j"),
-                    )
+                    copy(out=grouped[:, a, :, :], in_=e_banks[m, a][:].rearrange("p j r -> p r j"))
                 e_grouped[m] = grouped
 
             def quantise_e(m):
@@ -400,16 +395,12 @@ def tile_gatedcrossattention_pa_k_kernel(
                 next_tile += 1
                 scores_left = next_tile < T_TILES
                 if scores_left:
-                    score_group(next_tile, c * CHUNK_GROUPS)
-                    score_group(next_tile, c * CHUNK_GROUPS + 1)
+                    for g in range(c * CHUNK_GROUPS, (c + 1) * CHUNK_GROUPS):
+                        score_group(score_psum, next_tile, g)
                 if m < CHUNKS:
                     exp_chunk(m)
                 if 1 <= m <= CHUNKS:
                     turn_e(m - 1)
-                if scores_left:
-                    score_group(next_tile, c * CHUNK_GROUPS + 2)
-                    score_group(next_tile, c * CHUNK_GROUPS + 3)
-                if 1 <= m <= CHUNKS:
                     group_e(m - 1, scores_left)
                     if c == 0:
                         invert_sum(next_tile - 2)

@@ -26,6 +26,8 @@ CHUNK_GROUPS = 4
 CHUNK = CHUNK_GROUPS * K_PASS
 CHUNKS_PER_TILE = GROUPS // CHUNK_GROUPS
 CHUNKS = T_TILES * CHUNKS_PER_TILE
+BANK_GROUPS = 2
+CHUNK_BANKS = CHUNK_GROUPS // BANK_GROUPS
 GATE_LAG = 2
 
 FLOPS = 2 * (S * E * E + T * E * E + T * S * Z + T * S * E)
@@ -332,19 +334,33 @@ def tile_gatedcrossattention_pa_k_kernel(
                 inverse_sum[i] = inverse
 
             def turn_e(m):
-                for a in range(CHUNK_GROUPS):
-                    turned = e_psum.tile([P, PACK, P], BF16)
-                    for j in range(PACK):
-                        column = (a * PACK + j) * P
-                        nc.tensor.transpose(turned[:, j, :], e_rows[m][:, column : column + P], identity_bf16[:])
-                    e_banks[m, a] = turned
+                for b in range(CHUNK_BANKS):
+                    turned = e_psum.tile([P, BANK_GROUPS, PACK, P], BF16)
+                    for a in range(BANK_GROUPS):
+                        for j in range(PACK):
+                            column = ((b * BANK_GROUPS + a) * PACK + j) * P
+                            nc.tensor.transpose(turned[:, a, j, :], e_rows[m][:, column : column + P], identity_bf16[:])
+                    e_banks[m, b] = turned
 
             def group_e(m, scores_left):
                 grouped = work.tile([P, CHUNK_GROUPS, P, PACK], BF16, align_bytes=64)
-                for a in range(CHUNK_GROUPS):
-                    to_vector = a == CHUNK_GROUPS - 1 if scores_left else a > 0
-                    copy = nc.vector.tensor_copy if to_vector else nc.scalar.copy
-                    copy(out=grouped[:, a, :, :], in_=e_banks[m, a][:].rearrange("p j r -> p r j"))
+                for b in range(CHUNK_BANKS):
+                    groups = slice(b * BANK_GROUPS, (b + 1) * BANK_GROUPS)
+                    if scores_left:
+                        flat = work.tile([P, BANK_GROUPS, PACK, P], BF16, bufs=4)
+                        nc.scalar.copy(out=flat[:], in_=e_banks[m, b][:])
+                        nc.gpsimd.tensor_scalar(
+                            out=grouped[:, groups, :, :],
+                            in0=flat[:].rearrange("p a j r -> p a r j"),
+                            scalar1=1.0,
+                            scalar2=0.0,
+                            op0=ALU.mult,
+                            op1=ALU.add,
+                        )
+                    else:
+                        nc.vector.tensor_copy(
+                            out=grouped[:, groups, :, :], in_=e_banks[m, b][:].rearrange("p a j r -> p a r j")
+                        )
                 e_grouped[m] = grouped
 
             def quantise_e(m):

@@ -20,14 +20,17 @@ K_PASS = P * PACK
 T, S, E, Z = 640, 8192, 512, 128
 T_TILES = T // P
 GROUPS = S // K_PASS
+PAIRS = PACK // 2
 E_WORDS = E // 2
+TILES_PER_BANK = 2
+QUADRANT = 32
+SCALE_ROWS = 4
 N_BLOCKS = E // P
 CHUNK_GROUPS = 4
 CHUNK = CHUNK_GROUPS * K_PASS
 CHUNKS_PER_TILE = GROUPS // CHUNK_GROUPS
 CHUNKS = T_TILES * CHUNKS_PER_TILE
-BANK_GROUPS = 2
-CHUNK_BANKS = CHUNK_GROUPS // BANK_GROUPS
+KEY_AHEAD = 4
 GATE_LAG = 2
 
 FLOPS = 2 * (S * E * E + T * E * E + T * S * Z + T * S * E)
@@ -38,10 +41,10 @@ def load_weight(nc, pool, words, scales, label):
     plane = pool.tile([P, E], U8, name=label + "_plane", align_bytes=64)
     nc.vector.memset(plane[:].bitcast(I32), 0)
     scale_rows = scales.rearrange("g q n -> (g q) n").bitcast(I32)
-    for quadrant in range(4):
+    for quadrant in range(P // QUADRANT):
         nc.sync.dma_start(
-            out=plane[32 * quadrant : 32 * quadrant + 4, :].bitcast(I32),
-            in_=scale_rows[4 * quadrant : 4 * quadrant + 4, :],
+            out=plane[QUADRANT * quadrant : QUADRANT * quadrant + SCALE_ROWS, :].bitcast(I32),
+            in_=scale_rows[SCALE_ROWS * quadrant : SCALE_ROWS * (quadrant + 1), :],
         )
     nc.sync.dma_start(out=codes[:].bitcast(I32), in_=words.rearrange("g p n t -> (g p) (n t)").bitcast(I32))
     return codes, plane
@@ -61,12 +64,12 @@ def spread_bias(nc, pool, psum, ones, bias, label):
 def features_onto_partitions(nc, psum, identity_f32, rows, grouped, n_tiles):
     row_words = rows[:].bitcast(F32)
     grouped_words = grouped[:].bitcast(F32)
-    for first in range(0, n_tiles, 2):
-        count = min(2, n_tiles - first)
-        turned = psum.tile([P, 2, 2, P], F32, tag="turned")
+    for first in range(0, n_tiles, TILES_PER_BANK):
+        count = min(TILES_PER_BANK, n_tiles - first)
+        turned = psum.tile([P, TILES_PER_BANK, PAIRS, P], F32, tag="turned")
         for a in range(count):
-            for u in range(2):
-                nc.tensor.transpose(turned[:, a, u, :], row_words[:, first + a, u:E_WORDS:2], identity_f32[:])
+            for u in range(PAIRS):
+                nc.tensor.transpose(turned[:, a, u, :], row_words[:, first + a, u:E_WORDS:PAIRS], identity_f32[:])
         nc.scalar.copy(
             out=grouped_words[:, first : first + count, :, :],
             in_=turned[:, 0:count, :, :].rearrange("p a u r -> p a r u"),
@@ -95,6 +98,8 @@ def tile_gatedcrossattention_pa_k_kernel(
         make_identity(nc, identity_bf16[:])
         ones = const.tile([P, P], BF16)
         nc.vector.memset(ones[:], 1.0)
+        table_warmer = const.tile([P, 1], F32)
+        nc.scalar.activation(out=table_warmer[:], in_=ones[:, 0:1], func=FUNC.Silu)
 
         k_turned = keep.tile([P, S], BF16)
         q_turned = keep.tile([P, T], BF16)
@@ -136,9 +141,9 @@ def tile_gatedcrossattention_pa_k_kernel(
 
         with ExitStack() as value_phase:
             stage = value_phase.enter_context(tc.tile_pool(name="stage", bufs=2))
-            turn_psum = value_phase.enter_context(tc.psum_pool(name="turn_psum", bufs=2))
-            product_psum = value_phase.enter_context(tc.psum_pool(name="product_psum", bufs=4))
-            early_score_psum = value_phase.enter_context(tc.psum_pool(name="early_score_psum", bufs=2))
+            turn_psum = value_phase.enter_context(tc.psum_pool(name="turn_psum", bufs=3))
+            product_psum = value_phase.enter_context(tc.psum_pool(name="product_psum", bufs=N_BLOCKS))
+            early_score_psum = value_phase.enter_context(tc.psum_pool(name="early_score_psum", bufs=1))
 
             key_rows = {}
             key_grouped = {}
@@ -149,7 +154,7 @@ def tile_gatedcrossattention_pa_k_kernel(
             gate_f32 = {}
 
             def load_key(g):
-                rows = stage.tile([P, PACK, E], BF16, bufs=4)
+                rows = stage.tile([P, PACK, E], BF16, bufs=KEY_AHEAD)
                 nc.sync.dma_start(out=rows[:], in_=key_groups[g])
                 key_rows[g] = rows
 
@@ -245,9 +250,9 @@ def tile_gatedcrossattention_pa_k_kernel(
             def gate_silu(i):
                 nc.scalar.activation(out=gate[:, i, :], in_=gate_f32[i][:], func=FUNC.Silu)
 
+            load_key(0)
             bias_v = spread_bias(nc, const, product_psum, ones, bv, "bias_v")
             bias_r = spread_bias(nc, const, product_psum, ones, br, "bias_r")
-            load_key(0)
             wv_codes, wv_plane = load_weight(nc, const, Wv_words, Wv_scales, "wv")
             load_key(1)
             load_key(2)
@@ -280,10 +285,8 @@ def tile_gatedcrossattention_pa_k_kernel(
                     gate_silu(n - GATE_LAG - 1)
                 if n + 1 < GROUPS:
                     quantise_key(n + 1)
-                if n >= 1:
-                    score_group(early_score_psum, 0, n - 1)
-                if n + 4 < GROUPS:
-                    load_key(n + 4)
+                if n + KEY_AHEAD < GROUPS:
+                    load_key(n + KEY_AHEAD)
                 if n + 2 < GROUPS:
                     turn_key(n + 2)
                 if n == 0:
@@ -293,11 +296,12 @@ def tile_gatedcrossattention_pa_k_kernel(
                 if n == 1:
                     quantise_query()
                 if n >= 1:
+                    score_group(early_score_psum, 0, n - 1)
                     quantise_value(n - 1)
 
         with ExitStack() as softmax_phase:
             work = softmax_phase.enter_context(tc.tile_pool(name="work", bufs=3, reuse_waits="tile"))
-            e_psum = softmax_phase.enter_context(tc.psum_pool(name="e_psum", bufs=4, reuse_waits="tile"))
+            e_psum = softmax_phase.enter_context(tc.psum_pool(name="e_psum", bufs=CHUNK_GROUPS, reuse_waits="tile"))
             h_psum = softmax_phase.enter_context(tc.psum_pool(name="h_psum", bufs=1, reuse_waits="tile"))
             score_psum = softmax_phase.enter_context(tc.psum_pool(name="score_psum", bufs=3, reuse_waits="tile"))
 
@@ -334,33 +338,19 @@ def tile_gatedcrossattention_pa_k_kernel(
                 inverse_sum[i] = inverse
 
             def turn_e(m):
-                for b in range(CHUNK_BANKS):
-                    turned = e_psum.tile([P, BANK_GROUPS, PACK, P], BF16)
-                    for a in range(BANK_GROUPS):
-                        for j in range(PACK):
-                            column = ((b * BANK_GROUPS + a) * PACK + j) * P
-                            nc.tensor.transpose(turned[:, a, j, :], e_rows[m][:, column : column + P], identity_bf16[:])
-                    e_banks[m, b] = turned
+                for a in range(CHUNK_GROUPS):
+                    turned = e_psum.tile([P, PACK, P], BF16)
+                    for j in range(PACK):
+                        column = (a * PACK + j) * P
+                        nc.tensor.transpose(turned[:, j, :], e_rows[m][:, column : column + P], identity_bf16[:])
+                    e_banks[m, a] = turned
 
             def group_e(m, scores_left):
                 grouped = work.tile([P, CHUNK_GROUPS, P, PACK], BF16, align_bytes=64)
-                for b in range(CHUNK_BANKS):
-                    groups = slice(b * BANK_GROUPS, (b + 1) * BANK_GROUPS)
-                    if scores_left:
-                        flat = work.tile([P, BANK_GROUPS, PACK, P], BF16, bufs=4)
-                        nc.scalar.copy(out=flat[:], in_=e_banks[m, b][:])
-                        nc.gpsimd.tensor_scalar(
-                            out=grouped[:, groups, :, :],
-                            in0=flat[:].rearrange("p a j r -> p a r j"),
-                            scalar1=1.0,
-                            scalar2=0.0,
-                            op0=ALU.mult,
-                            op1=ALU.add,
-                        )
-                    else:
-                        nc.vector.tensor_copy(
-                            out=grouped[:, groups, :, :], in_=e_banks[m, b][:].rearrange("p a j r -> p a r j")
-                        )
+                for a in range(CHUNK_GROUPS):
+                    to_vector = a == CHUNK_GROUPS - 1 if scores_left else a > 0
+                    copy = nc.vector.tensor_copy if to_vector else nc.scalar.copy
+                    copy(out=grouped[:, a, :, :], in_=e_banks[m, a][:].rearrange("p j r -> p r j"))
                 e_grouped[m] = grouped
 
             def quantise_e(m):
@@ -417,11 +407,12 @@ def tile_gatedcrossattention_pa_k_kernel(
                     exp_chunk(m)
                 if 1 <= m <= CHUNKS:
                     turn_e(m - 1)
-                    group_e(m - 1, scores_left)
                     if c == 0:
                         invert_sum(next_tile - 2)
                 if 2 <= m <= CHUNKS + 1:
                     quantise_e(m - 2)
+                if 1 <= m <= CHUNKS:
+                    group_e(m - 1, scores_left)
                 if m >= 3:
                     attend(m - 3)
                     if (m - 3) % CHUNKS_PER_TILE == CHUNKS_PER_TILE - 1:

@@ -126,8 +126,8 @@ def tile_gatedcrossattention_pa_k_kernel(
                 stop=True,
             )
             nc.vector.tensor_scalar(
-                out=scores[i][:, g * K_PASS : (g + 1) * K_PASS],
-                in0=bank[:],
+                out=scores[i][:, g * K_PASS : (g + 1) * K_PASS].rearrange("q (u p e) -> q u p e", u=PAIRS, e=2),
+                in0=bank[:].rearrange("q (u e p) -> q u p e", u=PAIRS, e=2),
                 scalar1=1.0,
                 scalar2=None,
                 op0=ALU.mult,
@@ -301,7 +301,7 @@ def tile_gatedcrossattention_pa_k_kernel(
 
         with ExitStack() as softmax_phase:
             work = softmax_phase.enter_context(tc.tile_pool(name="work", bufs=3, reuse_waits="tile"))
-            e_psum = softmax_phase.enter_context(tc.psum_pool(name="e_psum", bufs=CHUNK_GROUPS, reuse_waits="tile"))
+            e_psum = softmax_phase.enter_context(tc.psum_pool(name="e_psum", bufs=4, reuse_waits="tile"))
             h_psum = softmax_phase.enter_context(tc.psum_pool(name="h_psum", bufs=1, reuse_waits="tile"))
             score_psum = softmax_phase.enter_context(tc.psum_pool(name="score_psum", bufs=3, reuse_waits="tile"))
 
@@ -338,19 +338,24 @@ def tile_gatedcrossattention_pa_k_kernel(
                 inverse_sum[i] = inverse
 
             def turn_e(m):
-                for a in range(CHUNK_GROUPS):
-                    turned = e_psum.tile([P, PACK, P], BF16)
-                    for j in range(PACK):
-                        column = (a * PACK + j) * P
-                        nc.tensor.transpose(turned[:, j, :], e_rows[m][:, column : column + P], identity_bf16[:])
+                words = e_rows[m][:].bitcast(F32)
+                for a in range(0, CHUNK_GROUPS, TILES_PER_BANK):
+                    turned = e_psum.tile([P, TILES_PER_BANK, PAIRS, P], F32)
+                    for b in range(TILES_PER_BANK):
+                        for u in range(PAIRS):
+                            column = ((a + b) * PAIRS + u) * P
+                            nc.tensor.transpose(turned[:, b, u, :], words[:, column : column + P], identity_f32[:])
                     e_banks[m, a] = turned
 
             def group_e(m, scores_left):
                 grouped = work.tile([P, CHUNK_GROUPS, P, PACK], BF16, align_bytes=64)
-                for a in range(CHUNK_GROUPS):
-                    to_vector = a == CHUNK_GROUPS - 1 if scores_left else a > 0
-                    copy = nc.vector.tensor_copy if to_vector else nc.scalar.copy
-                    copy(out=grouped[:, a, :, :], in_=e_banks[m, a][:].rearrange("p j r -> p r j"))
+                grouped_words = grouped[:].bitcast(F32)
+                for a in range(0, CHUNK_GROUPS, TILES_PER_BANK):
+                    copy = nc.scalar.copy if scores_left else nc.vector.tensor_copy
+                    copy(
+                        out=grouped_words[:, a : a + TILES_PER_BANK, :, :],
+                        in_=e_banks[m, a][:].rearrange("p b u r -> p b r u"),
+                    )
                 e_grouped[m] = grouped
 
             def quantise_e(m):

@@ -61,6 +61,17 @@ def spread_bias(nc, pool, psum, ones, bias, label):
     return spread
 
 
+def bias_columns(nc, pool, psum, identity_bf16, bias, label):
+    rows = pool.tile([P, P], BF16, name=label + "_rows")
+    nc.vector.memset(rows[:], 0.0)
+    nc.sync.dma_start(out=rows[0:N_BLOCKS, :], in_=bias.rearrange("(b p) -> b p", p=P))
+    bank = psum.tile([P, P], BF16, tag="product")
+    nc.tensor.transpose(bank[:], rows[:], identity_bf16[:])
+    columns = pool.tile([P, N_BLOCKS], F32, name=label)
+    nc.scalar.copy(out=columns[:], in_=bank[:, 0:N_BLOCKS])
+    return columns
+
+
 def features_onto_partitions(nc, psum, identity_f32, rows, grouped, n_tiles):
     row_words = rows[:].bitcast(F32)
     grouped_words = grouped[:].bitcast(F32)
@@ -141,15 +152,15 @@ def tile_gatedcrossattention_pa_k_kernel(
 
         with ExitStack() as value_phase:
             stage = value_phase.enter_context(tc.tile_pool(name="stage", bufs=2))
-            turn_psum = value_phase.enter_context(tc.psum_pool(name="turn_psum", bufs=3))
-            product_psum = value_phase.enter_context(tc.psum_pool(name="product_psum", bufs=N_BLOCKS))
+            turn_psum = value_phase.enter_context(tc.psum_pool(name="turn_psum", bufs=4))
+            product_psum = value_phase.enter_context(tc.psum_pool(name="product_psum", bufs=3))
             early_score_psum = value_phase.enter_context(tc.psum_pool(name="early_score_psum", bufs=1))
 
             key_rows = {}
             key_grouped = {}
             key_codes = {}
             key_plane = {}
-            v_f32 = {}
+            v_rows = {}
             v_grouped = {}
             gate_f32 = {}
 
@@ -159,8 +170,18 @@ def tile_gatedcrossattention_pa_k_kernel(
                 key_rows[g] = rows
 
             def turn_key(g):
-                grouped = stage.tile([P, PACK, P, PACK], BF16, tag="key_grouped", align_bytes=64)
-                features_onto_partitions(nc, turn_psum, identity_f32, key_rows[g], grouped, PACK)
+                grouped = stage.tile([P, PAIRS, P, 2, PACK], BF16, tag="key_grouped", align_bytes=64)
+                grouped_words = grouped[:].rearrange("p u r e t -> p u r (e t)").bitcast(F32)
+                row_words = key_rows[g][:].bitcast(F32)
+                for u in range(PAIRS):
+                    turned = turn_psum.tile([P, 2 * PAIRS, P], F32, tag="turned")
+                    for e in range(2):
+                        for w in range(PAIRS):
+                            nc.tensor.transpose(
+                                turned[:, e * PAIRS + w, :], row_words[:, 2 * u + e, w:E_WORDS:PAIRS], identity_f32[:]
+                            )
+                    copy = nc.vector.tensor_copy if u == 0 else nc.scalar.copy
+                    copy(out=grouped_words[:, u, :, :], in_=turned[:].rearrange("p s r -> p r s"))
                 key_grouped[g] = grouped
 
             def quantise_key(g):
@@ -169,7 +190,7 @@ def tile_gatedcrossattention_pa_k_kernel(
                 nc.vector.quantize_mx(
                     out=codes[:].bitcast(FP8X4),
                     scales=plane[:],
-                    in_=key_grouped[g][:].rearrange("p j r t -> p (j r t)"),
+                    in_=key_grouped[g][:].rearrange("p u r e t -> p (u r e t)"),
                 )
                 key_codes[g] = codes
                 key_plane[g] = plane
@@ -197,39 +218,45 @@ def tile_gatedcrossattention_pa_k_kernel(
                         in_=query_grouped[:, first : first + count, :, :].rearrange("p a r t -> p (a r t)"),
                     )
 
-            def value_products(g):
-                summed = stage.tile([P, N_BLOCKS, P, PACK], F32)
+            def values(g):
+                rows = stage.tile([P, N_BLOCKS, K_PASS], BF16, tag="v_rows")
                 for nb in range(N_BLOCKS):
                     features = slice(nb * P, (nb + 1) * P)
-                    product = product_psum.tile([P, PACK, P], F32)
-                    for j in range(PACK):
-                        slot = slice(j * P, (j + 1) * P)
-                        nc.tensor.matmul_mx(
-                            out=product[:, j, :],
-                            lhsT=key_codes[g][:, slot].bitcast(FP8X4),
-                            lhsT_scale=key_plane[g][:, slot],
-                            rhs=wv_codes[:, features].bitcast(FP8X4),
-                            rhs_scale=wv_plane[:, features],
-                            start=True,
-                            stop=True,
-                        )
-                    nc.vector.tensor_tensor(
-                        out=summed[:, nb, :, :],
-                        in0=product[:].rearrange("p j n -> p n j"),
-                        in1=bias_v[:, features].unsqueeze(2).to_broadcast([P, P, PACK]),
-                        op=ALU.add,
+                    product = product_psum.tile([P, K_PASS], F32)
+                    nc.tensor.matmul_mx(
+                        out=product[:],
+                        lhsT=wv_codes[:, features].bitcast(FP8X4),
+                        lhsT_scale=wv_plane[:, features],
+                        rhs=key_codes[g][:].bitcast(FP8X4),
+                        rhs_scale=key_plane[g][:],
+                        start=True,
+                        stop=True,
                     )
-                v_f32[g] = summed
+                    nc.scalar.activation(
+                        out=rows[:, nb, :], in_=product[:], func=FUNC.Silu, bias=bias_v[:, nb : nb + 1]
+                    )
+                v_rows[g] = rows
 
-            def value_silu(g):
-                grouped = stage.tile([P, E * PACK], BF16, tag="v_grouped", align_bytes=64)
-                nc.scalar.activation(
-                    out=grouped[:], in_=v_f32[g][:].rearrange("p b n j -> p (b n j)"), func=FUNC.Silu
-                )
+            def turn_value(g):
+                grouped = stage.tile([P, E, PACK], BF16, tag="v_grouped", align_bytes=64)
+                grouped_words = grouped[:].bitcast(F32)
+                row_words = v_rows[g][:].bitcast(F32)
+                for nb in range(0, N_BLOCKS, TILES_PER_BANK):
+                    turned = turn_psum.tile([P, TILES_PER_BANK, PAIRS, P], F32, tag="turned")
+                    for b in range(TILES_PER_BANK):
+                        for u in range(PAIRS):
+                            nc.tensor.transpose(
+                                turned[:, b, u, :], row_words[:, nb + b, u * P : (u + 1) * P], identity_f32[:]
+                            )
+                    features = slice(nb * P, (nb + TILES_PER_BANK) * P)
+                    nc.vector.tensor_copy(
+                        out=grouped_words[:, features, :].rearrange("p (b n) u -> p b n u", b=TILES_PER_BANK),
+                        in_=turned[:].rearrange("p b u n -> p b n u"),
+                    )
                 v_grouped[g] = grouped
 
             def quantise_value(g):
-                nc.vector.quantize_mx(out=v_codes[:, g, :].bitcast(FP8X4), scales=v_plane[:, g, :], in_=v_grouped[g][:])
+                nc.vector.quantize_mx(out=v_codes[:, g, :].bitcast(FP8X4), scales=v_plane[:, g, :], in_=v_grouped[g][:].rearrange("p n t -> p (n t)"))
 
             def gate_products(i):
                 queries = slice(i * P, (i + 1) * P)
@@ -251,7 +278,7 @@ def tile_gatedcrossattention_pa_k_kernel(
                 nc.scalar.activation(out=gate[:, i, :], in_=gate_f32[i][:], func=FUNC.Silu)
 
             load_key(0)
-            bias_v = spread_bias(nc, const, product_psum, ones, bv, "bias_v")
+            bias_v = bias_columns(nc, const, product_psum, identity_bf16, bv, "bias_v")
             bias_r = spread_bias(nc, const, product_psum, ones, br, "bias_r")
             wv_codes, wv_plane = load_weight(nc, const, Wv_words, Wv_scales, "wv")
             load_key(1)
@@ -276,17 +303,17 @@ def tile_gatedcrossattention_pa_k_kernel(
             quantise_key(0)
             for n in range(GROUPS + 1):
                 if n < GROUPS:
-                    value_products(n)
+                    values(n)
                 if GATE_LAG <= n < GATE_LAG + T_TILES:
                     gate_products(n - GATE_LAG)
-                if n >= 1:
-                    value_silu(n - 1)
                 if GATE_LAG + 1 <= n < GATE_LAG + 1 + T_TILES:
                     gate_silu(n - GATE_LAG - 1)
                 if n + 1 < GROUPS:
                     quantise_key(n + 1)
                 if n + KEY_AHEAD < GROUPS:
                     load_key(n + KEY_AHEAD)
+                if n >= 1:
+                    turn_value(n - 1)
                 if n + 2 < GROUPS:
                     turn_key(n + 2)
                 if n == 0:

@@ -119,16 +119,11 @@ def tile_gatedcrossattention_pa_k_kernel(
         gate = keep.tile([P, T_TILES, E], F32)
 
         scores = {}
+        score_bank = {}
         group_max = {}
         neg_max = {}
 
-        def score_group(score_psum, i, g):
-            if g == 0:
-                score_rows = score_pool.tile([P, S], F32)
-                scores[i] = score_rows
-                maxima = score_pool.tile([P, GROUPS], F32)
-                group_max[i] = maxima
-            bank = score_psum.tile([P, K_PASS], F32)
+        def score_matmul(bank, i, g):
             nc.tensor.matmul(
                 out=bank[:],
                 lhsT=q_turned[:, i * P : (i + 1) * P],
@@ -136,9 +131,17 @@ def tile_gatedcrossattention_pa_k_kernel(
                 start=True,
                 stop=True,
             )
+            score_bank[i, g] = bank
+
+        def score_out(i, g):
+            if g == 0:
+                score_rows = score_pool.tile([P, S], F32)
+                scores[i] = score_rows
+                maxima = score_pool.tile([P, GROUPS], F32)
+                group_max[i] = maxima
             nc.vector.tensor_scalar(
                 out=scores[i][:, g * K_PASS : (g + 1) * K_PASS].rearrange("q (u p e) -> q u p e", u=PAIRS, e=2),
-                in0=bank[:].rearrange("q (u e p) -> q u p e", u=PAIRS, e=2),
+                in0=score_bank[i, g][:].rearrange("q (u e p) -> q u p e", u=PAIRS, e=2),
                 scalar1=1.0,
                 scalar2=None,
                 op0=ALU.mult,
@@ -153,13 +156,13 @@ def tile_gatedcrossattention_pa_k_kernel(
         with ExitStack() as value_phase:
             stage = value_phase.enter_context(tc.tile_pool(name="stage", bufs=2))
             turn_psum = value_phase.enter_context(tc.psum_pool(name="turn_psum", bufs=4))
-            product_psum = value_phase.enter_context(tc.psum_pool(name="product_psum", bufs=3))
-            early_score_psum = value_phase.enter_context(tc.psum_pool(name="early_score_psum", bufs=1))
+            product_psum = value_phase.enter_context(tc.psum_pool(name="product_psum", bufs=N_BLOCKS))
 
             key_rows = {}
             key_grouped = {}
             key_codes = {}
             key_plane = {}
+            v_products = {}
             v_rows = {}
             v_grouped = {}
             gate_f32 = {}
@@ -169,7 +172,7 @@ def tile_gatedcrossattention_pa_k_kernel(
                 nc.sync.dma_start(out=rows[:], in_=key_groups[g])
                 key_rows[g] = rows
 
-            def turn_key(g):
+            def turn_key(g, copies):
                 grouped = stage.tile([P, PAIRS, P, 2, PACK], BF16, tag="key_grouped", align_bytes=64)
                 grouped_words = grouped[:].rearrange("p u r e t -> p u r (e t)").bitcast(F32)
                 row_words = key_rows[g][:].bitcast(F32)
@@ -180,8 +183,7 @@ def tile_gatedcrossattention_pa_k_kernel(
                             nc.tensor.transpose(
                                 turned[:, e * PAIRS + w, :], row_words[:, 2 * u + e, w:E_WORDS:PAIRS], identity_f32[:]
                             )
-                    copy = nc.vector.tensor_copy if u == 0 else nc.scalar.copy
-                    copy(out=grouped_words[:, u, :, :], in_=turned[:].rearrange("p s r -> p r s"))
+                    copies[u](out=grouped_words[:, u, :, :], in_=turned[:].rearrange("p s r -> p r s"))
                 key_grouped[g] = grouped
 
             def quantise_key(g):
@@ -218,8 +220,7 @@ def tile_gatedcrossattention_pa_k_kernel(
                         in_=query_grouped[:, first : first + count, :, :].rearrange("p a r t -> p (a r t)"),
                     )
 
-            def values(g):
-                rows = stage.tile([P, N_BLOCKS, K_PASS], BF16, tag="v_rows")
+            def value_products(g):
                 for nb in range(N_BLOCKS):
                     features = slice(nb * P, (nb + 1) * P)
                     product = product_psum.tile([P, K_PASS], F32)
@@ -232,10 +233,14 @@ def tile_gatedcrossattention_pa_k_kernel(
                         start=True,
                         stop=True,
                     )
-                    nc.scalar.activation(
-                        out=rows[:, nb, :], in_=product[:], func=FUNC.Silu, bias=bias_v[:, nb : nb + 1]
-                    )
+                    v_products[g, nb] = product
+                rows = stage.tile([P, N_BLOCKS, K_PASS], BF16, tag="v_rows")
                 v_rows[g] = rows
+
+            def value_silu(g, nb):
+                nc.scalar.activation(
+                    out=v_rows[g][:, nb, :], in_=v_products[g, nb][:], func=FUNC.Silu, bias=bias_v[:, nb : nb + 1]
+                )
 
             def turn_value(g):
                 grouped = stage.tile([P, E, PACK], BF16, tag="v_grouped", align_bytes=64)
@@ -249,7 +254,8 @@ def tile_gatedcrossattention_pa_k_kernel(
                                 turned[:, b, u, :], row_words[:, nb + b, u * P : (u + 1) * P], identity_f32[:]
                             )
                     features = slice(nb * P, (nb + TILES_PER_BANK) * P)
-                    nc.vector.tensor_copy(
+                    copy = nc.vector.tensor_copy if nb == 0 else nc.scalar.copy
+                    copy(
                         out=grouped_words[:, features, :].rearrange("p (b n) u -> p b n u", b=TILES_PER_BANK),
                         in_=turned[:].rearrange("p b u n -> p b n u"),
                     )
@@ -298,33 +304,41 @@ def tile_gatedcrossattention_pa_k_kernel(
             query_codes = stage.tile([P, T], U32, bufs=1, align_bytes=64)
             query_plane = stage.tile([P, T], U8, bufs=1, align_bytes=64)
 
-            turn_key(0)
-            turn_key(1)
-            quantise_key(0)
-            for n in range(GROUPS + 1):
+            for g in range(2):
+                turn_key(g, (nc.vector.tensor_copy, nc.scalar.copy))
+                quantise_key(g)
+            for n in range(GROUPS + 2):
+                gate_tile = n - GATE_LAG
                 if n < GROUPS:
-                    values(n)
-                if GATE_LAG <= n < GATE_LAG + T_TILES:
-                    gate_products(n - GATE_LAG)
-                if GATE_LAG + 1 <= n < GATE_LAG + 1 + T_TILES:
-                    gate_silu(n - GATE_LAG - 1)
-                if n + 1 < GROUPS:
-                    quantise_key(n + 1)
-                if n + KEY_AHEAD < GROUPS:
-                    load_key(n + KEY_AHEAD)
-                if n >= 1:
+                    value_products(n)
+                    for nb in range(N_BLOCKS - 1):
+                        value_silu(n, nb)
+                if 0 <= gate_tile < T_TILES:
+                    gate_products(gate_tile)
+                if 1 <= n <= GROUPS:
                     turn_value(n - 1)
-                if n + 2 < GROUPS:
-                    turn_key(n + 2)
+                if n < GROUPS:
+                    value_silu(n, N_BLOCKS - 1)
                 if n == 0:
                     turn_queries()
                 if n < GROUPS:
                     turn_k(n)
+                if 1 <= gate_tile <= T_TILES:
+                    gate_silu(gate_tile - 1)
+                if n >= 2:
+                    quantise_value(n - 2)
+                if n + KEY_AHEAD < GROUPS:
+                    load_key(n + KEY_AHEAD)
+                if n + 2 < GROUPS:
+                    turn_key(n + 2, (nc.vector.tensor_copy, nc.vector.tensor_copy))
                 if n == 1:
                     quantise_query()
-                if n >= 1:
-                    score_group(early_score_psum, 0, n - 1)
-                    quantise_value(n - 1)
+                if 1 <= n <= GROUPS:
+                    score_bank_0 = turn_psum.tile([P, K_PASS], F32, tag="turned")
+                    score_matmul(score_bank_0, 0, n - 1)
+                    score_out(0, n - 1)
+                if n + 2 < GROUPS:
+                    quantise_key(n + 2)
 
         with ExitStack() as softmax_phase:
             work = softmax_phase.enter_context(tc.tile_pool(name="work", bufs=3, reuse_waits="tile"))
@@ -434,7 +448,9 @@ def tile_gatedcrossattention_pa_k_kernel(
                 scores_left = next_tile < T_TILES
                 if scores_left:
                     for g in range(c * CHUNK_GROUPS, (c + 1) * CHUNK_GROUPS):
-                        score_group(score_psum, next_tile, g)
+                        bank = score_psum.tile([P, K_PASS], F32)
+                        score_matmul(bank, next_tile, g)
+                        score_out(next_tile, g)
                 if m < CHUNKS:
                     exp_chunk(m)
                 if 1 <= m <= CHUNKS:

@@ -29,9 +29,14 @@ N_BLOCKS = E // P
 CHUNK_GROUPS = 4
 CHUNK = CHUNK_GROUPS * K_PASS
 CHUNKS_PER_TILE = GROUPS // CHUNK_GROUPS
-CHUNKS = T_TILES * CHUNKS_PER_TILE
+WHOLE_CHUNKS = [(i, c * CHUNK_GROUPS, CHUNK_GROUPS) for i in range(T_TILES) for c in range(CHUNKS_PER_TILE)]
+CHUNKS = WHOLE_CHUNKS[:-1] + [
+    (T_TILES - 1, GROUPS - CHUNK_GROUPS, CHUNK_GROUPS // 2),
+    (T_TILES - 1, GROUPS - CHUNK_GROUPS // 2, CHUNK_GROUPS // 2),
+]
+LAST = len(CHUNKS) - 1
 KEY_AHEAD = 4
-GATE_LAG = 2
+GATE_LAG = 3
 
 FLOPS = 2 * (S * E * E + T * E * E + T * S * Z + T * S * E)
 
@@ -50,22 +55,22 @@ def load_weight(nc, pool, words, scales, label):
     return codes, plane
 
 
-def spread_bias(nc, pool, psum, ones, bias, label):
-    rows = pool.tile([P, E], BF16, name=label + "_rows")
+def load_bias_rows(nc, pool, bias, n_rows, label):
+    width = E // n_rows
+    rows = pool.tile([P, width], BF16, name=label)
     nc.vector.memset(rows[:], 0.0)
-    nc.sync.dma_start(out=rows[0:1, :], in_=bias.unsqueeze(0))
-    bank = psum.tile([P, E], F32, tag="product")
+    nc.sync.dma_start(out=rows[0:n_rows, :], in_=bias.rearrange("(b p) -> b p", p=width))
+    return rows
+
+
+def spread_bias(nc, pool, bank, ones, rows, label):
     nc.tensor.matmul(out=bank[:], lhsT=ones[:], rhs=rows[:], start=True, stop=True)
     spread = pool.tile([P, E], F32, name=label)
     nc.scalar.copy(out=spread[:], in_=bank[:])
     return spread
 
 
-def bias_columns(nc, pool, psum, identity_bf16, bias, label):
-    rows = pool.tile([P, P], BF16, name=label + "_rows")
-    nc.vector.memset(rows[:], 0.0)
-    nc.sync.dma_start(out=rows[0:N_BLOCKS, :], in_=bias.rearrange("(b p) -> b p", p=P))
-    bank = psum.tile([P, P], BF16, tag="product")
+def bias_columns(nc, pool, bank, identity_bf16, rows, label):
     nc.tensor.transpose(bank[:], rows[:], identity_bf16[:])
     columns = pool.tile([P, N_BLOCKS], F32, name=label)
     nc.scalar.copy(out=columns[:], in_=bank[:, 0:N_BLOCKS])
@@ -205,11 +210,13 @@ def tile_gatedcrossattention_pa_k_kernel(
                     out=k_turned[:, g * K_PASS : (g + 1) * K_PASS], in_=turned[:].rearrange("p j r -> p (j r)")
                 )
 
-            def turn_queries():
+            def turn_q():
                 q_bank = turn_psum.tile([P, T_TILES, P], BF16, tag="turned")
                 for i in range(T_TILES):
                     nc.tensor.transpose(q_bank[:, i, :], q_rows[:, i, :], identity_bf16[:])
                 nc.scalar.copy(out=q_turned[:], in_=q_bank[:].rearrange("p i r -> p (i r)"))
+
+            def turn_queries():
                 features_onto_partitions(nc, turn_psum, identity_f32, query_rows, query_grouped, T_TILES)
 
             def quantise_query():
@@ -220,8 +227,8 @@ def tile_gatedcrossattention_pa_k_kernel(
                         in_=query_grouped[:, first : first + count, :, :].rearrange("p a r t -> p (a r t)"),
                     )
 
-            def value_products(g):
-                for nb in range(N_BLOCKS):
+            def value_products(g, blocks):
+                for nb in blocks:
                     features = slice(nb * P, (nb + 1) * P)
                     product = product_psum.tile([P, K_PASS], F32)
                     nc.tensor.matmul_mx(
@@ -234,10 +241,11 @@ def tile_gatedcrossattention_pa_k_kernel(
                         stop=True,
                     )
                     v_products[g, nb] = product
-                rows = stage.tile([P, N_BLOCKS, K_PASS], BF16, tag="v_rows")
-                v_rows[g] = rows
 
             def value_silu(g, nb):
+                if nb == 0:
+                    rows = stage.tile([P, N_BLOCKS, K_PASS], BF16, tag="v_rows")
+                    v_rows[g] = rows
                 nc.scalar.activation(
                     out=v_rows[g][:, nb, :], in_=v_products[g, nb][:], func=FUNC.Silu, bias=bias_v[:, nb : nb + 1]
                 )
@@ -284,45 +292,60 @@ def tile_gatedcrossattention_pa_k_kernel(
                 nc.scalar.activation(out=gate[:, i, :], in_=gate_f32[i][:], func=FUNC.Silu)
 
             load_key(0)
-            bias_v = bias_columns(nc, const, product_psum, identity_bf16, bv, "bias_v")
-            bias_r = spread_bias(nc, const, product_psum, ones, br, "bias_r")
-            wv_codes, wv_plane = load_weight(nc, const, Wv_words, Wv_scales, "wv")
             load_key(1)
+            wv_codes, wv_plane = load_weight(nc, const, Wv_words, Wv_scales, "wv")
+            bias_v_rows = load_bias_rows(nc, const, bv, N_BLOCKS, "bias_v_rows")
+            q_rows = stage.tile([P, T_TILES, Z], BF16, bufs=1)
+            nc.sync.dma_start(out=q_rows[:], in_=q_tiles)
+            k_rows = stage.tile([P, GROUPS, PACK * Z], BF16, bufs=1)
+
+            def load_k(chunk):
+                groups = slice(chunk * CHUNK_GROUPS, (chunk + 1) * CHUNK_GROUPS)
+                nc.sync.dma_start(out=k_rows[:, groups, :], in_=k_groups[:, groups, :])
+
+            load_k(0)
             load_key(2)
             query_rows = stage.tile([P, T_TILES, E], BF16, bufs=1)
             nc.sync.dma_start(out=query_rows[:], in_=query_tiles)
             wr_codes, wr_plane = load_weight(nc, const, Wr_words, Wr_scales, "wr")
+            bias_r_rows = load_bias_rows(nc, const, br, 1, "bias_r_rows")
             load_key(3)
-            q_rows = stage.tile([P, T_TILES, Z], BF16, bufs=1)
-            nc.gpsimd.dma_start(out=q_rows[:], in_=q_tiles)
-            k_rows = stage.tile([P, GROUPS, PACK * Z], BF16, bufs=1)
-            for first in range(0, GROUPS, CHUNK_GROUPS):
-                nc.gpsimd.dma_start(
-                    out=k_rows[:, first : first + CHUNK_GROUPS, :], in_=k_groups[:, first : first + CHUNK_GROUPS, :]
-                )
+            for chunk in range(1, CHUNKS_PER_TILE):
+                load_k(chunk)
             query_grouped = stage.tile([P, T_TILES, P, PACK], BF16, bufs=1, align_bytes=64)
             query_codes = stage.tile([P, T], U32, bufs=1, align_bytes=64)
             query_plane = stage.tile([P, T], U8, bufs=1, align_bytes=64)
 
-            for g in range(2):
-                turn_key(g, (nc.vector.tensor_copy, nc.scalar.copy))
-                quantise_key(g)
+            turn_key(0, (nc.vector.tensor_copy, nc.scalar.copy))
+            bias_v_bank = product_psum.tile([P, P], BF16, tag="product")
+            bias_v = bias_columns(nc, const, bias_v_bank, identity_bf16, bias_v_rows, "bias_v")
+            quantise_key(0)
+            turn_key(1, (nc.vector.tensor_copy, nc.scalar.copy))
+            quantise_key(1)
             for n in range(GROUPS + 2):
                 gate_tile = n - GATE_LAG
                 if n < GROUPS:
-                    value_products(n)
-                    for nb in range(N_BLOCKS - 1):
-                        value_silu(n, nb)
-                if 0 <= gate_tile < T_TILES:
-                    gate_products(gate_tile)
+                    value_products(n, range(0, 2))
+                    value_silu(n, 0)
+                    value_silu(n, 1)
                 if 1 <= n <= GROUPS:
                     turn_value(n - 1)
-                if n < GROUPS:
-                    value_silu(n, N_BLOCKS - 1)
                 if n == 0:
-                    turn_queries()
+                    turn_q()
+                    turn_k(0)
+                if n + 1 < GROUPS:
+                    turn_k(n + 1)
                 if n < GROUPS:
-                    turn_k(n)
+                    value_products(n, range(2, N_BLOCKS))
+                    value_silu(n, 2)
+                    value_silu(n, 3)
+                if gate_tile == -1:
+                    bias_r_bank = product_psum.tile([P, E], F32, tag="product")
+                    bias_r = spread_bias(nc, const, bias_r_bank, ones, bias_r_rows, "bias_r")
+                if 0 <= gate_tile < T_TILES:
+                    gate_products(gate_tile)
+                if n == 1:
+                    turn_queries()
                 if 1 <= gate_tile <= T_TILES:
                     gate_silu(gate_tile - 1)
                 if n >= 2:
@@ -331,14 +354,16 @@ def tile_gatedcrossattention_pa_k_kernel(
                     load_key(n + KEY_AHEAD)
                 if n + 2 < GROUPS:
                     turn_key(n + 2, (nc.vector.tensor_copy, nc.vector.tensor_copy))
-                if n == 1:
+                if n == 2:
                     quantise_query()
-                if 1 <= n <= GROUPS:
+                if n < GROUPS:
                     score_bank_0 = turn_psum.tile([P, K_PASS], F32, tag="turned")
-                    score_matmul(score_bank_0, 0, n - 1)
-                    score_out(0, n - 1)
+                    score_matmul(score_bank_0, 0, n)
+                    score_out(0, n)
                 if n + 2 < GROUPS:
                     quantise_key(n + 2)
+                if n == GROUPS - 1:
+                    nc.scalar.activation(out=table_warmer[:], in_=ones[:, 0:1], func=FUNC.Exp)
 
         with ExitStack() as softmax_phase:
             work = softmax_phase.enter_context(tc.tile_pool(name="work", bufs=3, reuse_waits="tile"))
@@ -352,37 +377,42 @@ def tile_gatedcrossattention_pa_k_kernel(
             e_codes = {}
             e_plane = {}
             chunk_sum = {}
+            sums_of = {}
             inverse_sum = {}
             h_bank = {}
 
             def exp_chunk(m):
-                i, c = divmod(m, CHUNKS_PER_TILE)
-                if c == 0:
-                    sums = work.tile([P, CHUNKS_PER_TILE], F32, bufs=2)
+                i, first, count = CHUNKS[m]
+                if first == 0:
+                    sums = work.tile([P, GROUPS], F32, bufs=2)
                     chunk_sum[i] = sums
+                    sums_of[i] = 0
                 rows = work.tile([P, CHUNK], BF16)
                 nc.scalar.activation(
-                    out=rows[:],
-                    in_=scores[i][:, c * CHUNK : (c + 1) * CHUNK],
+                    out=rows[:, 0 : count * K_PASS],
+                    in_=scores[i][:, first * K_PASS : (first + count) * K_PASS],
                     func=FUNC.Exp,
                     bias=neg_max[i][:, 0:1],
                     scale=1.0,
-                    accum_out=chunk_sum[i][:, c : c + 1],
+                    accum_out=chunk_sum[i][:, sums_of[i] : sums_of[i] + 1],
                 )
+                sums_of[i] += 1
                 e_rows[m] = rows
 
             def invert_sum(i):
                 row_sum = work.tile([P, 1], F32)
-                nc.vector.tensor_reduce(out=row_sum[:], in_=chunk_sum[i][:], axis=AXIS.X, op=ALU.add)
+                nc.vector.tensor_reduce(out=row_sum[:], in_=chunk_sum[i][:, 0 : sums_of[i]], axis=AXIS.X, op=ALU.add)
                 inverse = work.tile([P, 1], F32)
                 nc.vector.reciprocal(out=inverse[:], in_=row_sum[:])
                 inverse_sum[i] = inverse
 
             def turn_e(m):
                 words = e_rows[m][:].bitcast(F32)
-                for a in range(0, CHUNK_GROUPS, TILES_PER_BANK):
+                count = CHUNKS[m][2]
+                in_bank = TILES_PER_BANK if m < LAST else 1
+                for a in range(0, count, in_bank):
                     turned = e_psum.tile([P, TILES_PER_BANK, PAIRS, P], F32)
-                    for b in range(TILES_PER_BANK):
+                    for b in range(in_bank):
                         for u in range(PAIRS):
                             column = ((a + b) * PAIRS + u) * P
                             nc.tensor.transpose(turned[:, b, u, :], words[:, column : column + P], identity_f32[:])
@@ -391,34 +421,37 @@ def tile_gatedcrossattention_pa_k_kernel(
             def group_e(m, scores_left):
                 grouped = work.tile([P, CHUNK_GROUPS, P, PACK], BF16, align_bytes=64)
                 grouped_words = grouped[:].bitcast(F32)
-                for a in range(0, CHUNK_GROUPS, TILES_PER_BANK):
-                    copy = nc.scalar.copy if scores_left else nc.vector.tensor_copy
+                count = CHUNKS[m][2]
+                in_bank = TILES_PER_BANK if m < LAST else 1
+                for a in range(0, count, in_bank):
+                    to_scalar = scores_left or (m == LAST and a == 0)
+                    copy = nc.scalar.copy if to_scalar else nc.vector.tensor_copy
                     copy(
-                        out=grouped_words[:, a : a + TILES_PER_BANK, :, :],
-                        in_=e_banks[m, a][:].rearrange("p b u r -> p b r u"),
+                        out=grouped_words[:, a : a + in_bank, :, :],
+                        in_=e_banks[m, a][:, 0:in_bank, :, :].rearrange("p b u r -> p b r u"),
                     )
                 e_grouped[m] = grouped
 
             def quantise_e(m):
-                i, c = divmod(m, CHUNKS_PER_TILE)
-                if c == 0:
+                i, first, count = CHUNKS[m]
+                if first == 0:
                     codes = work.tile([P, GROUPS * P], U32, bufs=2, align_bytes=64)
                     plane = work.tile([P, GROUPS * P], U8, bufs=2, align_bytes=64)
                     e_codes[i] = codes
                     e_plane[i] = plane
-                columns = slice(c * CHUNK_GROUPS * P, (c + 1) * CHUNK_GROUPS * P)
+                columns = slice(first * P, (first + count) * P)
                 nc.vector.quantize_mx(
                     out=e_codes[i][:, columns].bitcast(FP8X4),
                     scales=e_plane[i][:, columns],
-                    in_=e_grouped[m][:].rearrange("p a r j -> p (a r j)"),
+                    in_=e_grouped[m][:, 0:count, :, :].rearrange("p a r j -> p (a r j)"),
                 )
 
             def attend(m):
-                i, c = divmod(m, CHUNKS_PER_TILE)
-                if c == 0:
+                i, first, count = CHUNKS[m]
+                if first == 0:
                     bank = h_psum.tile([P, E], F32)
                     h_bank[i] = bank
-                for g in range(c * CHUNK_GROUPS, (c + 1) * CHUNK_GROUPS):
+                for g in range(first, first + count):
                     queries = slice(g * P, (g + 1) * P)
                     nc.tensor.matmul_mx(
                         out=h_bank[i][:],
@@ -429,20 +462,25 @@ def tile_gatedcrossattention_pa_k_kernel(
                         start=(g == 0),
                         stop=(g == GROUPS - 1),
                     )
+                if first + count == GROUPS:
+                    finish_tile(i)
 
             def finish_tile(i):
                 result = work.tile([P, E], F32, bufs=2)
-                nc.vector.scalar_tensor_tensor(
-                    out=result[:],
-                    in0=h_bank[i][:],
-                    scalar=inverse_sum[i][:, 0:1],
-                    in1=gate[:, i, :],
-                    op0=ALU.mult,
-                    op1=ALU.mult,
-                )
-                nc.sync.dma_start(out=out_tiles[i], in_=result[:])
+                width = E if i < T_TILES - 1 else E // 2
+                for column in range(0, E, width):
+                    features = slice(column, column + width)
+                    nc.vector.scalar_tensor_tensor(
+                        out=result[:, features],
+                        in0=h_bank[i][:, features],
+                        scalar=inverse_sum[i][:, 0:1],
+                        in1=gate[:, i, features],
+                        op0=ALU.mult,
+                        op1=ALU.mult,
+                    )
+                    nc.sync.dma_start(out=out_tiles[i][:, features], in_=result[:, features])
 
-            for m in range(CHUNKS + 3):
+            for m in range(LAST + 4):
                 next_tile, c = divmod(m, CHUNKS_PER_TILE)
                 next_tile += 1
                 scores_left = next_tile < T_TILES
@@ -451,17 +489,18 @@ def tile_gatedcrossattention_pa_k_kernel(
                         bank = score_psum.tile([P, K_PASS], F32)
                         score_matmul(bank, next_tile, g)
                         score_out(next_tile, g)
-                if m < CHUNKS:
-                    exp_chunk(m)
-                if 1 <= m <= CHUNKS:
-                    turn_e(m - 1)
-                    if c == 0:
-                        invert_sum(next_tile - 2)
-                if 2 <= m <= CHUNKS + 1:
-                    quantise_e(m - 2)
-                if 1 <= m <= CHUNKS:
-                    group_e(m - 1, scores_left)
-                if m >= 3:
+                elif m >= 3:
                     attend(m - 3)
-                    if (m - 3) % CHUNKS_PER_TILE == CHUNKS_PER_TILE - 1:
-                        finish_tile((m - 3) // CHUNKS_PER_TILE)
+                if m <= LAST:
+                    exp_chunk(m)
+                if 1 <= m <= LAST + 1:
+                    turn_e(m - 1)
+                if 2 <= m <= LAST + 2:
+                    quantise_e(m - 2)
+                if 1 <= m <= LAST + 1:
+                    group_e(m - 1, scores_left)
+                    i, first, count = CHUNKS[m - 1]
+                    if first + count == GROUPS:
+                        invert_sum(i)
+                if scores_left and m >= 3:
+                    attend(m - 3)

@@ -35,7 +35,7 @@ CHUNKS = WHOLE_CHUNKS[:-1] + [
     (T_TILES - 1, GROUPS - CHUNK_GROUPS // 2, CHUNK_GROUPS // 2),
 ]
 LAST = len(CHUNKS) - 1
-KEY_AHEAD = 4
+KEY_AHEAD = 5
 GATE_LAG = 3
 
 FLOPS = 2 * (S * E * E + T * E * E + T * S * Z + T * S * E)
@@ -164,6 +164,7 @@ def tile_gatedcrossattention_pa_k_kernel(
             product_psum = value_phase.enter_context(tc.psum_pool(name="product_psum", bufs=N_BLOCKS))
 
             key_rows = {}
+            key_words = {}
             key_grouped = {}
             key_codes = {}
             key_plane = {}
@@ -177,6 +178,15 @@ def tile_gatedcrossattention_pa_k_kernel(
                 nc.sync.dma_start(out=rows[:], in_=key_groups[g])
                 key_rows[g] = rows
 
+            def sort_key(g):
+                words = stage.tile([P, PACK, PAIRS, P], U32)
+                for j in range(PACK):
+                    nc.gpsimd.tensor_copy(
+                        out=words[:, j, :, :],
+                        in_=key_rows[g][:, j, :].bitcast(U32).rearrange("q (p w) -> q w p", w=PAIRS),
+                    )
+                key_words[g] = words[:].bitcast(F32)
+
             def turn_key(g, copies):
                 grouped = stage.tile([P, PAIRS, P, 2, PACK], BF16, tag="key_grouped", align_bytes=64)
                 grouped_words = grouped[:].rearrange("p u r e t -> p u r (e t)").bitcast(F32)
@@ -185,9 +195,8 @@ def tile_gatedcrossattention_pa_k_kernel(
                     turned = turn_psum.tile([P, 2 * PAIRS, P], F32, tag="turned")
                     for e in range(2):
                         for w in range(PAIRS):
-                            nc.tensor.transpose(
-                                turned[:, e * PAIRS + w, :], row_words[:, 2 * u + e, w:E_WORDS:PAIRS], identity_f32[:]
-                            )
+                            words = row_words[:, 2 * u + e, w:E_WORDS:PAIRS] if g < 2 else key_words[g][:, 2 * u + e, w, :]
+                            nc.tensor.transpose(turned[:, e * PAIRS + w, :], words, identity_f32[:])
                     copies[u](out=grouped_words[:, u, :, :], in_=turned[:].rearrange("p s r -> p r s"))
                 key_grouped[g] = grouped
 
@@ -250,7 +259,7 @@ def tile_gatedcrossattention_pa_k_kernel(
                     out=v_rows[g][:, nb, :], in_=v_products[g, nb][:], func=FUNC.Silu, bias=bias_v[:, nb : nb + 1]
                 )
 
-            def turn_value(g):
+            def turn_value(g, copies):
                 grouped = stage.tile([P, E, PACK], BF16, tag="v_grouped", align_bytes=64)
                 grouped_words = grouped[:].bitcast(F32)
                 row_words = v_rows[g][:].bitcast(F32)
@@ -262,8 +271,7 @@ def tile_gatedcrossattention_pa_k_kernel(
                                 turned[:, b, u, :], row_words[:, nb + b, u * P : (u + 1) * P], identity_f32[:]
                             )
                     features = slice(nb * P, (nb + TILES_PER_BANK) * P)
-                    copy = nc.vector.tensor_copy if nb == 0 else nc.scalar.copy
-                    copy(
+                    copies[nb // TILES_PER_BANK](
                         out=grouped_words[:, features, :].rearrange("p (b n) u -> p b n u", b=TILES_PER_BANK),
                         in_=turned[:].rearrange("p b u n -> p b n u"),
                     )
@@ -310,6 +318,7 @@ def tile_gatedcrossattention_pa_k_kernel(
             wr_codes, wr_plane = load_weight(nc, const, Wr_words, Wr_scales, "wr")
             bias_r_rows = load_bias_rows(nc, const, br, 1, "bias_r_rows")
             load_key(3)
+            load_key(4)
             for chunk in range(1, CHUNKS_PER_TILE):
                 load_k(chunk)
             query_grouped = stage.tile([P, T_TILES, P, PACK], BF16, bufs=1, align_bytes=64)
@@ -322,14 +331,17 @@ def tile_gatedcrossattention_pa_k_kernel(
             quantise_key(0)
             turn_key(1, (nc.vector.tensor_copy, nc.scalar.copy))
             quantise_key(1)
+            sort_key(2)
             for n in range(GROUPS + 2):
                 gate_tile = n - GATE_LAG
                 if n < GROUPS:
                     value_products(n, range(0, 2))
                     value_silu(n, 0)
                     value_silu(n, 1)
-                if 1 <= n <= GROUPS:
-                    turn_value(n - 1)
+                if 1 <= n < GROUPS:
+                    turn_value(n - 1, (nc.vector.tensor_copy, nc.scalar.copy))
+                if n == GROUPS:
+                    turn_value(n - 1, (nc.vector.tensor_copy, nc.vector.tensor_copy))
                 if n == 0:
                     turn_q()
                     turn_k(0)
@@ -350,6 +362,8 @@ def tile_gatedcrossattention_pa_k_kernel(
                     gate_silu(gate_tile - 1)
                 if n >= 2:
                     quantise_value(n - 2)
+                if n + 3 < GROUPS:
+                    sort_key(n + 3)
                 if n + KEY_AHEAD < GROUPS:
                     load_key(n + KEY_AHEAD)
                 if n + 2 < GROUPS:
@@ -424,7 +438,7 @@ def tile_gatedcrossattention_pa_k_kernel(
                 count = CHUNKS[m][2]
                 in_bank = TILES_PER_BANK if m < LAST else 1
                 for a in range(0, count, in_bank):
-                    to_scalar = scores_left or (m == LAST and a == 0)
+                    to_scalar = scores_left or m == LAST - 1 or (m == LAST and a == 0)
                     copy = nc.scalar.copy if to_scalar else nc.vector.tensor_copy
                     copy(
                         out=grouped_words[:, a : a + in_bank, :, :],
@@ -489,8 +503,6 @@ def tile_gatedcrossattention_pa_k_kernel(
                         bank = score_psum.tile([P, K_PASS], F32)
                         score_matmul(bank, next_tile, g)
                         score_out(next_tile, g)
-                elif m >= 3:
-                    attend(m - 3)
                 if m <= LAST:
                     exp_chunk(m)
                 if 1 <= m <= LAST + 1:
@@ -502,5 +514,5 @@ def tile_gatedcrossattention_pa_k_kernel(
                     i, first, count = CHUNKS[m - 1]
                     if first + count == GROUPS:
                         invert_sum(i)
-                if scores_left and m >= 3:
+                if m >= 3:
                     attend(m - 3)

from contextlib import ExitStack

import concourse.mybir as mybir
from concourse.masks import make_identity

F32 = mybir.dt.float32
BF16 = mybir.dt.bfloat16
I32 = mybir.dt.int32
U32 = mybir.dt.uint32
U8 = mybir.dt.uint8
FP8X4 = mybir.dt.float8_e4m3fn_x4
ALU = mybir.AluOpType
FUNC = mybir.ActivationFunctionType
AXIS = mybir.AxisListType

P = 128
PACK = 4
K_PASS = P * PACK

T, S, E, Z = 640, 8192, 512, 128
T_TILES = T // P
GROUPS = S // K_PASS
PAIRS = PACK // 2
E_WORDS = E // 2
TILES_PER_BANK = 2
QUADRANT = 32
SCALE_ROWS = 4
N_BLOCKS = E // P
CHUNK_GROUPS = 4
CHUNK = CHUNK_GROUPS * K_PASS
CHUNKS_PER_TILE = GROUPS // CHUNK_GROUPS
WHOLE_CHUNKS = [(i, c * CHUNK_GROUPS, CHUNK_GROUPS) for i in range(T_TILES) for c in range(CHUNKS_PER_TILE)]
CHUNKS = WHOLE_CHUNKS[:-1] + [
    (T_TILES - 1, GROUPS - CHUNK_GROUPS, CHUNK_GROUPS // 2),
    (T_TILES - 1, GROUPS - CHUNK_GROUPS // 2, CHUNK_GROUPS // 2),
]
LAST = len(CHUNKS) - 1
KEY_AHEAD = 5
GATE_LAG = 3

FLOPS = 2 * (S * E * E + T * E * E + T * S * Z + T * S * E)


def load_weight(nc, pool, words, scales, label):
    codes = pool.tile([P, E], U32, name=label + "_codes", align_bytes=64)
    plane = pool.tile([P, E], U8, name=label + "_plane", align_bytes=64)
    nc.vector.memset(plane[:].bitcast(I32), 0)
    scale_rows = scales.rearrange("g q n -> (g q) n").bitcast(I32)
    for quadrant in range(P // QUADRANT):
        nc.sync.dma_start(
            out=plane[QUADRANT * quadrant : QUADRANT * quadrant + SCALE_ROWS, :].bitcast(I32),
            in_=scale_rows[SCALE_ROWS * quadrant : SCALE_ROWS * (quadrant + 1), :],
        )
    nc.sync.dma_start(out=codes[:].bitcast(I32), in_=words.rearrange("g p n t -> (g p) (n t)").bitcast(I32))
    return codes, plane


def load_bias_rows(nc, pool, bias, n_rows, label):
    width = E // n_rows
    rows = pool.tile([P, width], BF16, name=label)
    nc.vector.memset(rows[:], 0.0)
    nc.sync.dma_start(out=rows[0:n_rows, :], in_=bias.rearrange("(b p) -> b p", p=width))
    return rows


def spread_bias(nc, pool, bank, ones, rows, label):
    nc.tensor.matmul(out=bank[:], lhsT=ones[:], rhs=rows[:], start=True, stop=True)
    spread = pool.tile([P, E], F32, name=label)
    nc.scalar.copy(out=spread[:], in_=bank[:])
    return spread


def bias_columns(nc, pool, bank, identity_bf16, rows, label):
    nc.tensor.transpose(bank[:], rows[:], identity_bf16[:])
    columns = pool.tile([P, N_BLOCKS], F32, name=label)
    nc.scalar.copy(out=columns[:], in_=bank[:, 0:N_BLOCKS])
    return columns


def features_onto_partitions(nc, psum, identity_f32, rows, grouped, n_tiles):
    row_words = rows[:].bitcast(F32)
    grouped_words = grouped[:].bitcast(F32)
    for first in range(0, n_tiles, TILES_PER_BANK):
        count = min(TILES_PER_BANK, n_tiles - first)
        turned = psum.tile([P, TILES_PER_BANK, PAIRS, P], F32, tag="turned")
        for a in range(count):
            for u in range(PAIRS):
                nc.tensor.transpose(turned[:, a, u, :], row_words[:, first + a, u:E_WORDS:PAIRS], identity_f32[:])
        nc.scalar.copy(
            out=grouped_words[:, first : first + count, :, :],
            in_=turned[:, 0:count, :, :].rearrange("p a u r -> p a r u"),
        )


def tile_gatedcrossattention_pa_k_kernel(
    tc, q_scaled, k, key, query, Wv_words, Wv_scales, bv, Wr_words, Wr_scales, br, out
):
    nc = tc.nc
    key_groups = key.rearrange("(g p j) b e -> g p j (b e)", p=P, j=PACK)
    k_groups = k.rearrange("(g p j) b z -> p g (j b z)", p=P, j=PACK)
    q_tiles = q_scaled.rearrange("(i p) b z -> p i (b z)", p=P)
    query_tiles = query.rearrange("(i p) b e -> p i (b e)", p=P)
    out_tiles = out.rearrange("(i p) b n -> i p (b n)", p=P)

    with ExitStack() as whole:
        const = whole.enter_context(tc.tile_pool(name="const", bufs=1))
        keep = whole.enter_context(tc.tile_pool(name="keep", bufs=1))
        score_pool = whole.enter_context(tc.tile_pool(name="score_pool", bufs=2))
        whole.enter_context(tc.manual_schedule())

        identity_f32 = const.tile([P, P], F32)
        make_identity(nc, identity_f32[:])
        identity_bf16 = const.tile([P, P], BF16)
        make_identity(nc, identity_bf16[:])
        ones = const.tile([P, P], BF16)
        nc.vector.memset(ones[:], 1.0)
        table_warmer = const.tile([P, 1], F32)
        nc.scalar.activation(out=table_warmer[:], in_=ones[:, 0:1], func=FUNC.Silu)

        k_turned = keep.tile([P, S], BF16)
        q_turned = keep.tile([P, T], BF16)
        v_codes = keep.tile([P, GROUPS, E], U32, align_bytes=64)
        v_plane = keep.tile([P, GROUPS, E], U8, align_bytes=64)
        gate = keep.tile([P, T_TILES, E], F32)

        scores = {}
        score_bank = {}
        group_max = {}
        neg_max = {}

        def score_matmul(bank, i, g):
            nc.tensor.matmul(
                out=bank[:],
                lhsT=q_turned[:, i * P : (i + 1) * P],
                rhs=k_turned[:, g * K_PASS : (g + 1) * K_PASS],
                start=True,
                stop=True,
            )
            score_bank[i, g] = bank

        def score_out(i, g):
            if g == 0:
                score_rows = score_pool.tile([P, S], F32)
                scores[i] = score_rows
                maxima = score_pool.tile([P, GROUPS], F32)
                group_max[i] = maxima
            nc.vector.tensor_scalar(
                out=scores[i][:, g * K_PASS : (g + 1) * K_PASS].rearrange("q (u p e) -> q u p e", u=PAIRS, e=2),
                in0=score_bank[i, g][:].rearrange("q (u e p) -> q u p e", u=PAIRS, e=2),
                scalar1=1.0,
                scalar2=None,
                op0=ALU.mult,
                op1=ALU.max,
                accum_out=group_max[i][:, g : g + 1],
            )
            if g == GROUPS - 1:
                minus_max = score_pool.tile([P, 1], F32)
                nc.vector.tensor_reduce(out=minus_max[:], in_=group_max[i][:], axis=AXIS.X, op=ALU.max, negate=True)
                neg_max[i] = minus_max

        with ExitStack() as value_phase:
            stage = value_phase.enter_context(tc.tile_pool(name="stage", bufs=2))
            turn_psum = value_phase.enter_context(tc.psum_pool(name="turn_psum", bufs=4))
            product_psum = value_phase.enter_context(tc.psum_pool(name="product_psum", bufs=N_BLOCKS))

            key_rows = {}
            key_words = {}
            key_grouped = {}
            key_codes = {}
            key_plane = {}
            v_products = {}
            v_rows = {}
            v_grouped = {}
            gate_f32 = {}

            def load_key(g):
                rows = stage.tile([P, PACK, E], BF16, bufs=KEY_AHEAD)
                nc.sync.dma_start(out=rows[:], in_=key_groups[g])
                key_rows[g] = rows

            def sort_key(g):
                words = stage.tile([P, PACK, PAIRS, P], U32)
                for j in range(PACK):
                    nc.gpsimd.tensor_copy(
                        out=words[:, j, :, :],
                        in_=key_rows[g][:, j, :].bitcast(U32).rearrange("q (p w) -> q w p", w=PAIRS),
                    )
                key_words[g] = words[:].bitcast(F32)

            def turn_key(g, copies):
                grouped = stage.tile([P, PAIRS, P, 2, PACK], BF16, tag="key_grouped", align_bytes=64)
                grouped_words = grouped[:].rearrange("p u r e t -> p u r (e t)").bitcast(F32)
                row_words = key_rows[g][:].bitcast(F32)
                for u in range(PAIRS):
                    turned = turn_psum.tile([P, 2 * PAIRS, P], F32, tag="turned")
                    for e in range(2):
                        for w in range(PAIRS):
                            words = row_words[:, 2 * u + e, w:E_WORDS:PAIRS] if g < 2 else key_words[g][:, 2 * u + e, w, :]
                            nc.tensor.transpose(turned[:, e * PAIRS + w, :], words, identity_f32[:])
                    copies[u](out=grouped_words[:, u, :, :], in_=turned[:].rearrange("p s r -> p r s"))
                key_grouped[g] = grouped

            def quantise_key(g):
                codes = stage.tile([P, K_PASS], U32, align_bytes=64)
                plane = stage.tile([P, K_PASS], U8, align_bytes=64)
                nc.vector.quantize_mx(
                    out=codes[:].bitcast(FP8X4),
                    scales=plane[:],
                    in_=key_grouped[g][:].rearrange("p u r e t -> p (u r e t)"),
                )
                key_codes[g] = codes
                key_plane[g] = plane

            def turn_k(g):
                turned = turn_psum.tile([P, PACK, P], BF16, tag="turned")
                for j in range(PACK):
                    nc.tensor.transpose(turned[:, j, :], k_rows[:, g, j * Z : (j + 1) * Z], identity_bf16[:])
                nc.scalar.copy(
                    out=k_turned[:, g * K_PASS : (g + 1) * K_PASS], in_=turned[:].rearrange("p j r -> p (j r)")
                )

            def turn_q():
                q_bank = turn_psum.tile([P, T_TILES, P], BF16, tag="turned")
                for i in range(T_TILES):
                    nc.tensor.transpose(q_bank[:, i, :], q_rows[:, i, :], identity_bf16[:])
                nc.scalar.copy(out=q_turned[:], in_=q_bank[:].rearrange("p i r -> p (i r)"))

            def turn_queries():
                features_onto_partitions(nc, turn_psum, identity_f32, query_rows, query_grouped, T_TILES)

            def quantise_query():
                for first, count in ((0, 4), (4, 1)):
                    nc.vector.quantize_mx(
                        out=query_codes[:, first * P : (first + count) * P].bitcast(FP8X4),
                        scales=query_plane[:, first * P : (first + count) * P],
                        in_=query_grouped[:, first : first + count, :, :].rearrange("p a r t -> p (a r t)"),
                    )

            def value_products(g, blocks):
                for nb in blocks:
                    features = slice(nb * P, (nb + 1) * P)
                    product = product_psum.tile([P, K_PASS], F32)
                    nc.tensor.matmul_mx(
                        out=product[:],
                        lhsT=wv_codes[:, features].bitcast(FP8X4),
                        lhsT_scale=wv_plane[:, features],
                        rhs=key_codes[g][:].bitcast(FP8X4),
                        rhs_scale=key_plane[g][:],
                        start=True,
                        stop=True,
                    )
                    v_products[g, nb] = product

            def value_silu(g, nb):
                if nb == 0:
                    rows = stage.tile([P, N_BLOCKS, K_PASS], BF16, tag="v_rows")
                    v_rows[g] = rows
                nc.scalar.activation(
                    out=v_rows[g][:, nb, :], in_=v_products[g, nb][:], func=FUNC.Silu, bias=bias_v[:, nb : nb + 1]
                )

            def turn_value(g, copies):
                grouped = stage.tile([P, E, PACK], BF16, tag="v_grouped", align_bytes=64)
                grouped_words = grouped[:].bitcast(F32)
                row_words = v_rows[g][:].bitcast(F32)
                for nb in range(0, N_BLOCKS, TILES_PER_BANK):
                    turned = turn_psum.tile([P, TILES_PER_BANK, PAIRS, P], F32, tag="turned")
                    for b in range(TILES_PER_BANK):
                        for u in range(PAIRS):
                            nc.tensor.transpose(
                                turned[:, b, u, :], row_words[:, nb + b, u * P : (u + 1) * P], identity_f32[:]
                            )
                    features = slice(nb * P, (nb + TILES_PER_BANK) * P)
                    copies[nb // TILES_PER_BANK](
                        out=grouped_words[:, features, :].rearrange("p (b n) u -> p b n u", b=TILES_PER_BANK),
                        in_=turned[:].rearrange("p b u n -> p b n u"),
                    )
                v_grouped[g] = grouped

            def quantise_value(g):
                nc.vector.quantize_mx(out=v_codes[:, g, :].bitcast(FP8X4), scales=v_plane[:, g, :], in_=v_grouped[g][:].rearrange("p n t -> p (n t)"))

            def gate_products(i):
                queries = slice(i * P, (i + 1) * P)
                product = product_psum.tile([P, E], F32, tag="product")
                nc.tensor.matmul_mx(
                    out=product[:],
                    lhsT=query_codes[:, queries].bitcast(FP8X4),
                    lhsT_scale=query_plane[:, queries],
                    rhs=wr_codes[:].bitcast(FP8X4),
                    rhs_scale=wr_plane[:],
                    start=True,
                    stop=True,
                )
                summed = stage.tile([P, E], F32, tag="gate_sum")
                nc.vector.tensor_tensor(out=summed[:], in0=product[:], in1=bias_r[:], op=ALU.add)
                gate_f32[i] = summed

            def gate_silu(i):
                nc.scalar.activation(out=gate[:, i, :], in_=gate_f32[i][:], func=FUNC.Silu)

            load_key(0)
            load_key(1)
            wv_codes, wv_plane = load_weight(nc, const, Wv_words, Wv_scales, "wv")
            bias_v_rows = load_bias_rows(nc, const, bv, N_BLOCKS, "bias_v_rows")
            q_rows = stage.tile([P, T_TILES, Z], BF16, bufs=1)
            nc.sync.dma_start(out=q_rows[:], in_=q_tiles)
            k_rows = stage.tile([P, GROUPS, PACK * Z], BF16, bufs=1)

            def load_k(chunk):
                groups = slice(chunk * CHUNK_GROUPS, (chunk + 1) * CHUNK_GROUPS)
                nc.sync.dma_start(out=k_rows[:, groups, :], in_=k_groups[:, groups, :])

            load_k(0)
            load_key(2)
            query_rows = stage.tile([P, T_TILES, E], BF16, bufs=1)
            nc.sync.dma_start(out=query_rows[:], in_=query_tiles)
            wr_codes, wr_plane = load_weight(nc, const, Wr_words, Wr_scales, "wr")
            bias_r_rows = load_bias_rows(nc, const, br, 1, "bias_r_rows")
            load_key(3)
            load_key(4)
            for chunk in range(1, CHUNKS_PER_TILE):
                load_k(chunk)
            query_grouped = stage.tile([P, T_TILES, P, PACK], BF16, bufs=1, align_bytes=64)
            query_codes = stage.tile([P, T], U32, bufs=1, align_bytes=64)
            query_plane = stage.tile([P, T], U8, bufs=1, align_bytes=64)

            turn_key(0, (nc.vector.tensor_copy, nc.scalar.copy))
            bias_v_bank = product_psum.tile([P, P], BF16, tag="product")
            bias_v = bias_columns(nc, const, bias_v_bank, identity_bf16, bias_v_rows, "bias_v")
            quantise_key(0)
            turn_key(1, (nc.vector.tensor_copy, nc.scalar.copy))
            quantise_key(1)
            sort_key(2)
            for n in range(GROUPS + 2):
                gate_tile = n - GATE_LAG
                if n < GROUPS:
                    value_products(n, range(0, 2))
                    value_silu(n, 0)
                    value_silu(n, 1)
                if 1 <= n < GROUPS:
                    turn_value(n - 1, (nc.vector.tensor_copy, nc.scalar.copy))
                if n == GROUPS:
                    turn_value(n - 1, (nc.vector.tensor_copy, nc.vector.tensor_copy))
                if n == 0:
                    turn_q()
                    turn_k(0)
                if n + 1 < GROUPS:
                    turn_k(n + 1)
                if n < GROUPS:
                    value_products(n, range(2, N_BLOCKS))
                    value_silu(n, 2)
                    value_silu(n, 3)
                if gate_tile == -1:
                    bias_r_bank = product_psum.tile([P, E], F32, tag="product")
                    bias_r = spread_bias(nc, const, bias_r_bank, ones, bias_r_rows, "bias_r")
                if 0 <= gate_tile < T_TILES:
                    gate_products(gate_tile)
                if n == 1:
                    turn_queries()
                if 1 <= gate_tile <= T_TILES:
                    gate_silu(gate_tile - 1)
                if n >= 2:
                    quantise_value(n - 2)
                if n + 3 < GROUPS:
                    sort_key(n + 3)
                if n + KEY_AHEAD < GROUPS:
                    load_key(n + KEY_AHEAD)
                if n + 2 < GROUPS:
                    turn_key(n + 2, (nc.vector.tensor_copy, nc.vector.tensor_copy))
                if n == 2:
                    quantise_query()
                if n < GROUPS:
                    score_bank_0 = turn_psum.tile([P, K_PASS], F32, tag="turned")
                    score_matmul(score_bank_0, 0, n)
                    score_out(0, n)
                if n + 2 < GROUPS:
                    quantise_key(n + 2)
                if n == GROUPS - 1:
                    nc.scalar.activation(out=table_warmer[:], in_=ones[:, 0:1], func=FUNC.Exp)

        with ExitStack() as softmax_phase:
            work = softmax_phase.enter_context(tc.tile_pool(name="work", bufs=3, reuse_waits="tile"))
            e_psum = softmax_phase.enter_context(tc.psum_pool(name="e_psum", bufs=4, reuse_waits="tile"))
            h_psum = softmax_phase.enter_context(tc.psum_pool(name="h_psum", bufs=1, reuse_waits="tile"))
            score_psum = softmax_phase.enter_context(tc.psum_pool(name="score_psum", bufs=3, reuse_waits="tile"))

            e_rows = {}
            e_banks = {}
            e_grouped = {}
            e_codes = {}
            e_plane = {}
            chunk_sum = {}
            sums_of = {}
            inverse_sum = {}
            h_bank = {}

            def exp_chunk(m):
                i, first, count = CHUNKS[m]
                if first == 0:
                    sums = work.tile([P, GROUPS], F32, bufs=2)
                    chunk_sum[i] = sums
                    sums_of[i] = 0
                rows = work.tile([P, CHUNK], BF16)
                nc.scalar.activation(
                    out=rows[:, 0 : count * K_PASS],
                    in_=scores[i][:, first * K_PASS : (first + count) * K_PASS],
                    func=FUNC.Exp,
                    bias=neg_max[i][:, 0:1],
                    scale=1.0,
                    accum_out=chunk_sum[i][:, sums_of[i] : sums_of[i] + 1],
                )
                sums_of[i] += 1
                e_rows[m] = rows

            def invert_sum(i):
                row_sum = work.tile([P, 1], F32)
                nc.vector.tensor_reduce(out=row_sum[:], in_=chunk_sum[i][:, 0 : sums_of[i]], axis=AXIS.X, op=ALU.add)
                inverse = work.tile([P, 1], F32)
                nc.vector.reciprocal(out=inverse[:], in_=row_sum[:])
                inverse_sum[i] = inverse

            def turn_e(m):
                words = e_rows[m][:].bitcast(F32)
                count = CHUNKS[m][2]
                in_bank = TILES_PER_BANK if m < LAST else 1
                for a in range(0, count, in_bank):
                    turned = e_psum.tile([P, TILES_PER_BANK, PAIRS, P], F32)
                    for b in range(in_bank):
                        for u in range(PAIRS):
                            column = ((a + b) * PAIRS + u) * P
                            nc.tensor.transpose(turned[:, b, u, :], words[:, column : column + P], identity_f32[:])
                    e_banks[m, a] = turned

            def group_e(m, scores_left):
                grouped = work.tile([P, CHUNK_GROUPS, P, PACK], BF16, align_bytes=64)
                grouped_words = grouped[:].bitcast(F32)
                count = CHUNKS[m][2]
                in_bank = TILES_PER_BANK if m < LAST else 1
                for a in range(0, count, in_bank):
                    to_scalar = scores_left or m == LAST - 1 or (m == LAST and a == 0)
                    copy = nc.scalar.copy if to_scalar else nc.vector.tensor_copy
                    copy(
                        out=grouped_words[:, a : a + in_bank, :, :],
                        in_=e_banks[m, a][:, 0:in_bank, :, :].rearrange("p b u r -> p b r u"),
                    )
                e_grouped[m] = grouped

            def quantise_e(m):
                i, first, count = CHUNKS[m]
                if first == 0:
                    codes = work.tile([P, GROUPS * P], U32, bufs=2, align_bytes=64)
                    plane = work.tile([P, GROUPS * P], U8, bufs=2, align_bytes=64)
                    e_codes[i] = codes
                    e_plane[i] = plane
                columns = slice(first * P, (first + count) * P)
                nc.vector.quantize_mx(
                    out=e_codes[i][:, columns].bitcast(FP8X4),
                    scales=e_plane[i][:, columns],
                    in_=e_grouped[m][:, 0:count, :, :].rearrange("p a r j -> p (a r j)"),
                )

            def attend(m):
                i, first, count = CHUNKS[m]
                if first == 0:
                    bank = h_psum.tile([P, E], F32)
                    h_bank[i] = bank
                for g in range(first, first + count):
                    queries = slice(g * P, (g + 1) * P)
                    nc.tensor.matmul_mx(
                        out=h_bank[i][:],
                        lhsT=e_codes[i][:, queries].bitcast(FP8X4),
                        lhsT_scale=e_plane[i][:, queries],
                        rhs=v_codes[:, g, :].bitcast(FP8X4),
                        rhs_scale=v_plane[:, g, :],
                        start=(g == 0),
                        stop=(g == GROUPS - 1),
                    )
                if first + count == GROUPS:
                    finish_tile(i)

            def finish_tile(i):
                result = work.tile([P, E], F32, bufs=2)
                width = E if i < T_TILES - 1 else E // 2
                for column in range(0, E, width):
                    features = slice(column, column + width)
                    nc.vector.scalar_tensor_tensor(
                        out=result[:, features],
                        in0=h_bank[i][:, features],
                        scalar=inverse_sum[i][:, 0:1],
                        in1=gate[:, i, features],
                        op0=ALU.mult,
                        op1=ALU.mult,
                    )
                    nc.sync.dma_start(out=out_tiles[i][:, features], in_=result[:, features])

            for m in range(LAST + 4):
                next_tile, c = divmod(m, CHUNKS_PER_TILE)
                next_tile += 1
                scores_left = next_tile < T_TILES
                if scores_left:
                    for g in range(c * CHUNK_GROUPS, (c + 1) * CHUNK_GROUPS):
                        bank = score_psum.tile([P, K_PASS], F32)
                        score_matmul(bank, next_tile, g)
                        score_out(next_tile, g)
                if m <= LAST:
                    exp_chunk(m)
                if 1 <= m <= LAST + 1:
                    turn_e(m - 1)
                if 2 <= m <= LAST + 2:
                    quantise_e(m - 2)
                if 1 <= m <= LAST + 1:
                    group_e(m - 1, scores_left)
                    i, first, count = CHUNKS[m - 1]
                    if first + count == GROUPS:
                        invert_sum(i)
                if m >= 3:
                    attend(m - 3)
